import numpy as np
import ml_dtypes


def mxq(x, axis, fmt="e4m3"):
    dtype, down = {"e4m3": (ml_dtypes.float8_e4m3fn, 7), "e5m2": (ml_dtypes.float8_e5m2, 14)}[fmt]
    v = np.moveaxis(np.asarray(x, np.float32).astype(ml_dtypes.bfloat16).astype(np.float64), axis, -1)
    blocks = v.reshape(v.shape[:-1] + (-1, 32))
    amax = np.abs(blocks).max(-1, keepdims=True)
    byte = np.maximum(np.where(amax > 0, np.frexp(amax)[1] - 1 + 127, 0) - down, 1)
    scale = np.exp2(byte - 127.0)
    codes = (blocks / scale).astype(np.float32).astype(dtype).astype(np.float64)
    return np.moveaxis((codes * scale).reshape(v.shape), -1, axis)


WIDE = False


def mx_kscale(k):
    if not WIDE:
        return np.ones(k)
    levels = np.array([10, -10, 5, -5, 0])
    a = np.random.permutation(np.resize(levels, k // 512 * 4)).reshape(k // 512, 4)
    idx = np.arange(k)
    return np.exp2(a[idx // 512, idx % 128 // 32])


BF16 = ml_dtypes.bfloat16


def bf(x):
    return np.asarray(x, np.float32).astype(BF16)


def f64(x):
    return np.asarray(x).astype(np.float64)


N, D, B = 1024, 512, 768


def setup_inputs():
    f = np.concatenate([np.ones(B), mx_kscale(N)[B:]])
    g = np.mean(f)
    return {"adjacency_matrix": bf(np.random.uniform(size=(N, N)) * f[None, :]),
            "node_features": bf(np.random.standard_normal((N, D)) / f[:, None]),
            "W_gcn": bf(np.random.standard_normal((D, D)) * 0.25 * np.sqrt(N) / np.sqrt(D) * g),
            "W_skip": bf(np.random.standard_normal((D, D)) * 0.5 / np.sqrt(D)),
            "batch_size": B}


def reference(adjacency_matrix, node_features, W_gcn, W_skip, batch_size):
    beta = 0.5
    a = f64(adjacency_matrix)
    x = f64(node_features)
    deg = np.sum(a, axis=1)
    d_inv_sqrt = 1.0 / np.sqrt(deg + 1e-8)
    normalized_adj = d_inv_sqrt[:, None] * a * d_inv_sqrt[None, :]
    h = x @ f64(W_gcn).T
    adj_rows = normalized_adj[:batch_size]
    gcn_out = np.maximum((mxq(adj_rows, 1, "e4m3") @ mxq(h, 0, "e4m3")) + x[:batch_size] @ f64(W_skip).T, 0.0)
    sample_features = gcn_out[:batch_size]
    original_features = x[:batch_size]
    enhanced_features = original_features + beta * sample_features
    return enhanced_features

@@ -1,0 +1,323 @@
+from contextlib import ExitStack
+
+import concourse.mybir as mybir
+from concourse.masks import make_identity
+
+F32 = mybir.dt.float32
+BF16 = mybir.dt.bfloat16
+U32 = mybir.dt.uint32
+U8 = mybir.dt.uint8
+FP8X4 = mybir.dt.float8_e4m3fn_x4
+ALU = mybir.AluOpType
+ACT = mybir.ActivationFunctionType
+
+P = 128
+N_NODES = 1024
+D = 512
+B = 768
+FLOPS = 2 * (B * N_NODES * D + N_NODES * D * D + B * D * D)
+CHUNKS = [(0, 0), (0, 1), (1, 0), (1, 1)]
+
+
+def tile_structureawaregcn_kernel(tc, adjacency_matrix, node_features, W_gcn, W_skip, batch_size, out):
+    nc = tc.nc
+    assert batch_size == B
+    with ExitStack() as ctx:
+        keep = ctx.enter_context(tc.tile_pool(name="keep", bufs=1))
+        scratch = ctx.enter_context(tc.tile_pool(name="scratch", bufs=2))
+        tp_pool = ctx.enter_context(tc.psum_pool(name="tp", bufs=3))
+        acc_pool = ctx.enter_context(tc.psum_pool(name="acc", bufs=3))
+        dj_pool = ctx.enter_context(tc.psum_pool(name="dj", bufs=1))
+        ctx.enter_context(tc.manual_schedule())
+
+        ident_f = keep.tile([P, P], F32, name="ident_f")
+        make_identity(nc, ident_f[:])
+        ident_b = keep.tile([P, P], BF16, name="ident_b")
+        make_identity(nc, ident_b[:])
+        warm = keep.tile([P, 1], F32, name="warm")
+        nc.vector.memset(warm[:], 1.0)
+        nc.scalar.sqrt(warm[:], warm[:])
+
+        def load(name, width, view, src):
+            t = keep.tile([P, width], BF16, name=name)
+            nc.sync.dma_start(out=t[:] if view is None else t[:].rearrange("p (a b) -> p a b", a=view), in_=src)
+            return t
+
+        wg_sb = load("wg_sb", 4 * D, 4, W_gcn.rearrange("(m p) c -> p m c", p=P))
+        x0_sb = load("x0_sb", 4 * D, 4, node_features[0:512, :].rearrange("(p t) c -> p t c", t=4))
+        a_rows = []
+        a03_src = adjacency_matrix[0:512, :].rearrange("(p t) j -> p t j", t=4)
+        for half in range(2):
+            a03 = load("a03_%d" % half, 2 * N_NODES, 2, a03_src[:, 2 * half : 2 * half + 2, :])
+            a_rows.append(a03[:, 0:N_NODES])
+            a_rows.append(a03[:, N_NODES : 2 * N_NODES])
+        for m in range(4, 8):
+            a47 = load("a47_%d" % m, N_NODES, None, adjacency_matrix[P * m : P * (m + 1), :])
+            a_rows.append(a47[:])
+        x1_sb = load("x1_sb", 4 * D, 4, node_features[512:1024, :].rearrange("(p t) c -> p t c", t=4))
+        ws_sb = load("ws_sb", 4 * D, 4, W_skip.rearrange("(m p) c -> p m c", p=P))
+        x45_sb = load("x45_sb", 2 * D, 2, node_features[512:768, :].rearrange("(m p) c -> p m c", p=P))
+
+        def new_words(name, blocks):
+            return keep.tile([P, 2 * blocks * P], F32, name=name)
+
+        def pairs(dst):
+            return dst[:].bitcast(BF16).rearrange("q (u n e) -> q u n e", u=2, e=2)
+
+        def t_w(src, blocks, u):
+            words = src[:].bitcast(F32)
+            bank = tp_pool.tile([P, blocks * P], F32, name="tpw", tag="tp")
+            for b in range(blocks):
+                nc.tensor.transpose(bank[:, b * P : (b + 1) * P], words[:, b * 256 + u * P : b * 256 + (u + 1) * P], ident_f[:])
+            return bank
+
+        def c_w(bank, dst, blocks, u, eng):
+            dst_u = dst[:, u * blocks * P : (u + 1) * blocks * P]
+            if eng == "v":
+                nc.vector.tensor_copy(out=dst_u, in_=bank[:])
+            else:
+                nc.scalar.copy(out=dst_u, in_=bank[:])
+
+        hgrp = [keep.tile([P, 4 * D], BF16, name="hgrp%d" % g, align_bytes=64) for g in range(2)]
+        hcodes = [keep.tile([P, D], U32, name="hcodes%d" % g, align_bytes=64) for g in range(2)]
+        hscales = [keep.tile([P, D], U8, name="hscales%d" % g, align_bytes=64) for g in range(2)]
+
+        def h_mm(xt, wt, oc):
+            bank = acc_pool.tile([P, 4 * P], F32, name="hacc", tag="acc")
+            for t in range(4):
+                for ci, (u, e) in enumerate(CHUNKS):
+                    nc.tensor.matmul(
+                        bank[:, t * P : (t + 1) * P],
+                        lhsT=xt[:, u, t * P : (t + 1) * P, e],
+                        rhs=wt[:, u, oc * P : (oc + 1) * P, e],
+                        start=(ci == 0),
+                        stop=(ci == 3),
+                    )
+            return bank
+
+        def h_out(bank, g, oc):
+            nc.scalar.copy(
+                out=hgrp[g][:, oc * 512 : (oc + 1) * 512].rearrange("p (o t) -> p o t", t=4),
+                in_=bank[:].rearrange("p (t o) -> p o t", t=4),
+            )
+
+        def q_h(g):
+            nc.vector.quantize_mx(out=hcodes[g][:].bitcast(FP8X4), scales=hscales[g][:], in_=hgrp[g][:])
+
+        def deg_v(tile_idx, dst):
+            rows = a_rows[tile_idx]
+            junk = scratch.tile([P, 512], F32, name="junk")
+            nc.vector.scalar_tensor_tensor(
+                out=junk[:], in0=rows[:, 0:512], scalar=1.0, in1=rows[:, 512:1024],
+                op0=ALU.mult, op1=ALU.add, accum_out=dst,
+            )
+
+        def deg_s(tile_idx, dst):
+            junk_s = scratch.tile([P, N_NODES], BF16, name="junk_s")
+            nc.scalar.activation(out=junk_s[:], in_=a_rows[tile_idx], func=ACT.Copy, accum_out=dst)
+
+        rec = [keep.tile([P, 4], F32, name="rec%d" % h) for h in range(2)]
+        dcol = [keep.tile([P, 4], F32, name="dcol%d" % h) for h in range(2)]
+        drep = [keep.tile([P, 4 * P], F32, name="drep%d" % h) for h in range(2)]
+        dj = [dj_pool.tile([P, 4 * P], F32, name="dj%d" % h) for h in range(2)]
+
+        def d_rep(h):
+            nc.scalar.activation(
+                out=drep[h][:].rearrange("p (k r) -> p k r", k=4),
+                in_=rec[h][:].unsqueeze(2).to_broadcast([P, 4, P]),
+                func=ACT.Sqrt,
+            )
+            nc.scalar.sqrt(dcol[h][:], rec[h][:])
+
+        def t_dj(h, col_of):
+            for k in range(4):
+                c = col_of[k]
+                nc.tensor.transpose(dj[h][:, k * P : (k + 1) * P], drep[h][:, c * P : (c + 1) * P], ident_f[:])
+
+        ahat = [keep.tile([P, N_NODES], BF16, name="ahat%d" % m) for m in range(6)]
+        COL0 = [0, 2, 1, 3]
+        COL1 = [0, 1, 2, 3]
+
+        def sc(m, g):
+            in1 = dj[g][:].rearrange("i (t p) -> i t p", t=4) if g == 0 else dj[g][:].rearrange("i (p t) -> i t p", t=4)
+            c = COL0[m] if m < 4 else COL1[m - 4]
+            nc.vector.scalar_tensor_tensor(
+                out=ahat[m][:, g * 512 : (g + 1) * 512].rearrange("i (t p) -> i t p", t=4),
+                in0=a_rows[m][:, g * 512 : (g + 1) * 512].rearrange("i (p t) -> i t p", t=4),
+                scalar=dcol[m // 4][:, c : c + 1],
+                in1=in1,
+                op0=ALU.mult,
+                op1=ALU.mult,
+            )
+
+        agrp = [keep.tile([P, N_NODES], BF16, name="agrp%d" % m, align_bytes=64) for m in range(6)]
+        acodes = [keep.tile([P, 256], U32, name="acodes%d" % m, align_bytes=64) for m in range(6)]
+        ascales = [keep.tile([P, 256], U8, name="ascales%d" % m, align_bytes=64) for m in range(6)]
+        skip_sb = [keep.tile([P, D], F32, name="skip%d" % m) for m in range(6)]
+        pre = [keep.tile([P, D], F32, name="pre%d" % m) for m in range(6)]
+        fin = [keep.tile([P, D], F32, name="fin%d" % m) for m in range(6)]
+
+        def at_one(bank, m, b):
+            nc.tensor.transpose(bank[:, b * P : (b + 1) * P], ahat[m][:, b * P : (b + 1) * P], ident_b[:])
+
+        def at(m):
+            bank = tp_pool.tile([P, N_NODES], BF16, name="tpa", tag="tp")
+            for b in range(8):
+                at_one(bank, m, b)
+            return bank
+
+        def a_out(bank, m):
+            nc.scalar.copy(
+                out=agrp[m][:].rearrange("p (g i t) -> p g i t", g=2, t=4),
+                in_=bank[:].rearrange("p (g t i) -> p g i t", g=2, t=4),
+            )
+
+        def q_a(m):
+            nc.vector.quantize_mx(out=acodes[m][:].bitcast(FP8X4), scales=ascales[m][:], in_=agrp[m][:])
+
+        def sk(m, xt0, xt45, wsT, weave):
+            xt, col = (xt0, m * P) if m < 4 else (xt45, (m - 4) * P)
+            sacc = acc_pool.tile([P, D], F32, name="sacc", tag="acc")
+            bank = None
+            if weave is not None:
+                bank = tp_pool.tile([P, N_NODES], BF16, name="tpa", tag="tp")
+            for ci, (u, e) in enumerate(CHUNKS):
+                nc.tensor.matmul(sacc[:], lhsT=xt[:, u, col : col + P, e], rhs=wsT[:, u, :, e], start=(ci == 0), stop=(ci == 3))
+                if weave is not None:
+                    at_one(bank, weave, 2 * ci)
+                    at_one(bank, weave, 2 * ci + 1)
+            return sacc, bank
+
+        def s_out(sacc, m):
+            nc.scalar.activation(out=skip_sb[m][:], in_=sacc[:], func=ACT.Copy, scale=0.5)
+
+        def mx(m):
+            macc = acc_pool.tile([P, D], F32, name="macc", tag="acc")
+            for g in range(2):
+                nc.tensor.matmul_mx(
+                    out=macc[:],
+                    lhsT=acodes[m][:, g * P : (g + 1) * P].bitcast(FP8X4),
+                    lhsT_scale=ascales[m][:, g * P : (g + 1) * P],
+                    rhs=hcodes[g][:].bitcast(FP8X4),
+                    rhs_scale=hscales[g][:],
+                    start=(g == 0),
+                    stop=(g == 1),
+                )
+            return macc
+
+        out03 = out[0:512, :].rearrange("(p t) o -> p t o", t=4)
+
+        def ep(macc, m):
+            nc.vector.scalar_tensor_tensor(out=pre[m][:], in0=macc[:], scalar=0.5, in1=skip_sb[m][:], op0=ALU.mult, op1=ALU.add)
+            res = x0_sb[:, m * D : (m + 1) * D] if m < 4 else x45_sb[:, (m - 4) * D : (m - 3) * D]
+            nc.vector.scalar_tensor_tensor(out=fin[m][:], in0=pre[m][:], scalar=0.0, in1=res, op0=ALU.max, op1=ALU.add)
+            dst = out03[:, m, :] if m < 4 else out[P * m : P * (m + 1), :]
+            nc.sync.dma_start(out=dst, in_=fin[m][:])
+
+        wgT_w = new_words("wgT", 4)
+        xt0_w = new_words("xt0", 4)
+        xt1_w = new_words("xt1", 4)
+        wsT_w = new_words("wsT", 4)
+        xt45_w = new_words("xt45", 2)
+        wgT, xt0, xt1, wsT, xt45 = pairs(wgT_w), pairs(xt0_w), pairs(xt1_w), pairs(wsT_w), pairs(xt45_w)
+        deg_v0 = keep.tile([P, 2], F32, name="deg_v0")
+        deg_s0 = keep.tile([P, 2], F32, name="deg_s0")
+        deg_v1 = keep.tile([P, 4], F32, name="deg_v1")
+
+        c_w(t_w(wg_sb, 4, 0), wgT_w, 4, 0, "v")
+        c_w(t_w(wg_sb, 4, 1), wgT_w, 4, 1, "s")
+        c_w(t_w(x0_sb, 4, 0), xt0_w, 4, 0, "v")
+        c_w(t_w(x0_sb, 4, 1), xt0_w, 4, 1, "s")
+        b0 = h_mm(xt0, wgT, 0)
+        deg_v(0, deg_v0[:, 0:1])
+        deg_s(1, deg_s0[:, 0:1])
+        h_out(b0, 0, 0)
+        b1 = h_mm(xt0, wgT, 1)
+        deg_v(2, deg_v0[:, 1:2])
+        deg_s(3, deg_s0[:, 1:2])
+        h_out(b1, 0, 1)
+        b2 = h_mm(xt0, wgT, 2)
+        deg_v(4, deg_v1[:, 0:1])
+        deg_v(5, deg_v1[:, 1:2])
+        nc.vector.tensor_scalar_add(rec[0][:, 0:2], deg_v0[:], 1e-8)
+        nc.vector.tensor_scalar_add(rec[0][:, 2:4], deg_s0[:], 1e-8)
+        nc.vector.reciprocal(rec[0][:], rec[0][:])
+        d_rep(0)
+        h_out(b2, 0, 2)
+        b3 = h_mm(xt0, wgT, 3)
+        deg_v(6, deg_v1[:, 2:3])
+        deg_v(7, deg_v1[:, 3:4])
+        nc.vector.tensor_scalar_add(rec[1][:], deg_v1[:], 1e-8)
+        nc.vector.reciprocal(rec[1][:], rec[1][:])
+        h_out(b3, 0, 3)
+        t_dj(0, COL0)
+        c_w(t_w(x1_sb, 4, 0), xt1_w, 4, 0, "s")
+        c_w(t_w(x1_sb, 4, 1), xt1_w, 4, 1, "s")
+        w0 = t_w(ws_sb, 4, 0)
+        w1 = t_w(ws_sb, 4, 1)
+        for m in range(4):
+            sc(m, 0)
+        d_rep(1)
+        c_w(w0, wsT_w, 4, 0, "s")
+        c_w(w1, wsT_w, 4, 1, "s")
+        b0 = h_mm(xt1, wgT, 0)
+        t_dj(1, COL1)
+        q_h(0)
+        h_out(b0, 1, 0)
+        b1 = h_mm(xt1, wgT, 1)
+        sc(0, 1)
+        h_out(b1, 1, 1)
+        t0 = at(0)
+        sc(1, 1)
+        a_out(t0, 0)
+        b2 = h_mm(xt1, wgT, 2)
+        h_out(b2, 1, 2)
+        t1 = at(1)
+        sc(2, 1)
+        a_out(t1, 1)
+        b3 = h_mm(xt1, wgT, 3)
+        h_out(b3, 1, 3)
+        t2 = at(2)
+        sc(3, 1)
+        q_a(0)
+        a_out(t2, 2)
+        c_w(t_w(x45_sb, 2, 0), xt45_w, 2, 0, "s")
+        c_w(t_w(x45_sb, 2, 1), xt45_w, 2, 1, "s")
+        t3 = at(3)
+        sc(4, 0)
+        sc(4, 1)
+        q_a(1)
+        a_out(t3, 3)
+        q_h(1)
+        s0, t4 = sk(0, xt0, xt45, wsT, 4)
+        s_out(s0, 0)
+        sc(5, 0)
+        sc(5, 1)
+        q_a(2)
+        a_out(t4, 4)
+        s1, t5 = sk(1, xt0, xt45, wsT, 5)
+        s_out(s1, 1)
+        q_a(3)
+        a_out(t5, 5)
+        m0 = mx(0)
+        m1 = mx(1)
+        ep(m0, 0)
+        s2, unused = sk(2, xt0, xt45, wsT, None)
+        s_out(s2, 2)
+        q_a(4)
+        m2 = mx(2)
+        ep(m1, 1)
+        s3, unused = sk(3, xt0, xt45, wsT, None)
+        s_out(s3, 3)
+        q_a(5)
+        m3 = mx(3)
+        ep(m2, 2)
+        s4, unused = sk(4, xt0, xt45, wsT, None)
+        s_out(s4, 4)
+        m4 = mx(4)
+        ep(m3, 3)
+        s5, unused = sk(5, xt0, xt45, wsT, None)
+        s_out(s5, 5)
+        m5 = mx(5)
+        ep(m4, 4)
+        ep(m5, 5)

@@ -25,10 +25,11 @@ def tile_structureawaregcn_kernel(tc, adjacency_matrix, node_features, W_gcn, W_
     with ExitStack() as ctx:
         keep = ctx.enter_context(tc.tile_pool(name="keep", bufs=1))
         scratch = ctx.enter_context(tc.tile_pool(name="scratch", bufs=2))
-        tp_pool = ctx.enter_context(tc.psum_pool(name="tp", bufs=3))
-        acc_pool = ctx.enter_context(tc.psum_pool(name="acc", bufs=3))
-        dj_pool = ctx.enter_context(tc.psum_pool(name="dj", bufs=1))
+        psum = ctx.enter_context(tc.psum_pool(name="psum", bufs=1))
         ctx.enter_context(tc.manual_schedule())
+
+        def bank(i, dtype):
+            return psum.tile([P, 512 if dtype == F32 else 1024], dtype, name="bk%d" % i, tag="bk%d" % i)
 
         ident_f = keep.tile([P, P], F32, name="ident_f")
         make_identity(nc, ident_f[:])
@@ -38,68 +39,88 @@ def tile_structureawaregcn_kernel(tc, adjacency_matrix, node_features, W_gcn, W_
         nc.vector.memset(warm[:], 1.0)
         nc.scalar.sqrt(warm[:], warm[:])
 
-        def load(name, width, view, src):
-            t = keep.tile([P, width], BF16, name=name)
-            nc.sync.dma_start(out=t[:] if view is None else t[:].rearrange("p (a b) -> p a b", a=view), in_=src)
-            return t
+        x_lo = node_features[0:512, :].rearrange("(p t) c -> p t c", t=4)
+        x_hi = node_features[512:1024, :].rearrange("(p t) c -> p t c", t=4)
+        a_lo = adjacency_matrix[0:512, :].rearrange("(p t) j -> p t j", t=4)
+        SRC = {
+            "wg0": W_gcn[0:256, :].rearrange("(m p) c -> p m c", p=P),
+            "wg1": W_gcn[256:512, :].rearrange("(m p) c -> p m c", p=P),
+            "ws0": W_skip[0:256, :].rearrange("(m p) c -> p m c", p=P),
+            "ws1": W_skip[256:512, :].rearrange("(m p) c -> p m c", p=P),
+            "x00": x_lo[:, 0:2, :],
+            "x01": x_lo[:, 2:4, :],
+            "x10": x_hi[:, 0:2, :],
+            "x11": x_hi[:, 2:4, :],
+            "x45": node_features[512:768, :].rearrange("(m p) c -> p m c", p=P),
+            "a03_0": a_lo[:, 0:2, :],
+            "a03_1": a_lo[:, 2:4, :],
+        }
+        T = {}
+        a_rows = {}
 
-        wg_sb = load("wg_sb", 4 * D, 4, W_gcn.rearrange("(m p) c -> p m c", p=P))
-        x0_sb = load("x0_sb", 4 * D, 4, node_features[0:512, :].rearrange("(p t) c -> p t c", t=4))
-        a_rows = []
-        a03_src = adjacency_matrix[0:512, :].rearrange("(p t) j -> p t j", t=4)
-        for half in range(2):
-            a03 = load("a03_%d" % half, 2 * N_NODES, 2, a03_src[:, 2 * half : 2 * half + 2, :])
-            a_rows.append(a03[:, 0:N_NODES])
-            a_rows.append(a03[:, N_NODES : 2 * N_NODES])
-        for m in range(4, 8):
-            a47 = load("a47_%d" % m, N_NODES, None, adjacency_matrix[P * m : P * (m + 1), :])
-            a_rows.append(a47[:])
-        x1_sb = load("x1_sb", 4 * D, 4, node_features[512:1024, :].rearrange("(p t) c -> p t c", t=4))
-        ws_sb = load("ws_sb", 4 * D, 4, W_skip.rearrange("(m p) c -> p m c", p=P))
-        x45_sb = load("x45_sb", 2 * D, 2, node_features[512:768, :].rearrange("(m p) c -> p m c", p=P))
-
-        def new_words(name, blocks):
-            return keep.tile([P, 2 * blocks * P], F32, name=name)
+        def ld(key):
+            if key in SRC:
+                src = SRC[key]
+                width = src.shape[1] * src.shape[2]
+                t = keep.tile([P, width], BF16, name="in_" + key)
+                nc.sync.dma_start(out=t[:].rearrange("p (a b) -> p a b", a=2), in_=src)
+                if key == "a03_0" or key == "a03_1":
+                    first = 0 if key == "a03_0" else 2
+                    a_rows[first] = t[:, 0:N_NODES]
+                    a_rows[first + 1] = t[:, N_NODES : 2 * N_NODES]
+            else:
+                m = int(key[1:])
+                t = keep.tile([P, N_NODES], BF16, name="in_" + key)
+                nc.sync.dma_start(out=t[:], in_=adjacency_matrix[P * m : P * (m + 1), :])
+                a_rows[m] = t[:]
+            T[key] = t
 
         def pairs(dst):
             return dst[:].bitcast(BF16).rearrange("q (u n e) -> q u n e", u=2, e=2)
 
-        def t_w(src, blocks, u):
+        def t_pair(src, bk):
             words = src[:].bitcast(F32)
-            bank = tp_pool.tile([P, blocks * P], F32, name="tpw", tag="tp")
-            for b in range(blocks):
-                nc.tensor.transpose(bank[:, b * P : (b + 1) * P], words[:, b * 256 + u * P : b * 256 + (u + 1) * P], ident_f[:])
-            return bank
+            for u in range(2):
+                for b in range(2):
+                    k = 2 * u + b
+                    nc.tensor.transpose(bk[:, k * P : (k + 1) * P], words[:, b * 256 + u * P : b * 256 + (u + 1) * P], ident_f[:])
 
-        def c_w(bank, dst, blocks, u, eng):
-            dst_u = dst[:, u * blocks * P : (u + 1) * blocks * P]
-            if eng == "v":
-                nc.vector.tensor_copy(out=dst_u, in_=bank[:])
+        def c_pair(bk, key, eng):
+            if key == "ws0" or key == "ws1":
+                b0 = 0 if key == "ws0" else 2
+                dst_v = wsT_w[:].rearrange("q (u n) -> q u n", u=2)[:, :, b0 * P : (b0 + 2) * P]
+                src_v = bk[:].rearrange("q (u n) -> q u n", u=2)
             else:
-                nc.scalar.copy(out=dst_u, in_=bank[:])
+                dst_v = WORDS[key][:]
+                src_v = bk[:]
+            if eng == "v":
+                nc.vector.tensor_copy(out=dst_v, in_=src_v)
+            else:
+                nc.scalar.copy(out=dst_v, in_=src_v)
 
         hgrp = [keep.tile([P, 4 * D], BF16, name="hgrp%d" % g, align_bytes=64) for g in range(2)]
         hcodes = [keep.tile([P, D], U32, name="hcodes%d" % g, align_bytes=64) for g in range(2)]
         hscales = [keep.tile([P, D], U8, name="hscales%d" % g, align_bytes=64) for g in range(2)]
 
-        def h_mm(xt, wt, oc):
-            bank = acc_pool.tile([P, 4 * P], F32, name="hacc", tag="acc")
-            for t in range(4):
-                for ci, (u, e) in enumerate(CHUNKS):
-                    nc.tensor.matmul(
-                        bank[:, t * P : (t + 1) * P],
-                        lhsT=xt[:, u, t * P : (t + 1) * P, e],
-                        rhs=wt[:, u, oc * P : (oc + 1) * P, e],
-                        start=(ci == 0),
-                        stop=(ci == 3),
-                    )
-            return bank
+        def h_grp(bk, g, t, oc):
+            xt = PAIRS["x%d%d" % (g, t // 2)]
+            wt = PAIRS["wg%d" % (oc // 2)]
+            for ci, (u, e) in enumerate(CHUNKS):
+                nc.tensor.matmul(
+                    bk[:, t * P : (t + 1) * P],
+                    lhsT=xt[:, u, (t % 2) * P : (t % 2 + 1) * P, e],
+                    rhs=wt[:, u, (oc % 2) * P : (oc % 2 + 1) * P, e],
+                    start=(ci == 0),
+                    stop=(ci == 3),
+                )
 
-        def h_out(bank, g, oc):
-            nc.scalar.copy(
-                out=hgrp[g][:, oc * 512 : (oc + 1) * 512].rearrange("p (o t) -> p o t", t=4),
-                in_=bank[:].rearrange("p (t o) -> p o t", t=4),
-            )
+        def h_out(bk, g, oc, eng):
+            dst_v = hgrp[g][:, oc * 512 : (oc + 1) * 512].rearrange("p (o t) -> p o t", t=4)
+            src_v = bk[:].rearrange("p (t o) -> p o t", t=4)
+            if eng == "v":
+                nc.vector.tensor_copy(out=dst_v, in_=src_v)
+            else:
+                nc.scalar.copy(out=dst_v, in_=src_v)
 
         def q_h(g):
             nc.vector.quantize_mx(out=hcodes[g][:].bitcast(FP8X4), scales=hscales[g][:], in_=hgrp[g][:])
@@ -112,6 +133,10 @@ def tile_structureawaregcn_kernel(tc, adjacency_matrix, node_features, W_gcn, W_
                 op0=ALU.mult, op1=ALU.add, accum_out=dst,
             )
 
+        def deg_f(tile_idx, dst):
+            junk_b = scratch.tile([P, N_NODES], BF16, name="junk_b")
+            nc.vector.tensor_scalar(out=junk_b[:], in0=a_rows[tile_idx], scalar1=1.0, scalar2=None, op0=ALU.mult, op1=ALU.add, accum_out=dst)
+
         def deg_s(tile_idx, dst):
             junk_s = scratch.tile([P, N_NODES], BF16, name="junk_s")
             nc.scalar.activation(out=junk_s[:], in_=a_rows[tile_idx], func=ACT.Copy, accum_out=dst)
@@ -119,7 +144,7 @@ def tile_structureawaregcn_kernel(tc, adjacency_matrix, node_features, W_gcn, W_
         rec = [keep.tile([P, 4], F32, name="rec%d" % h) for h in range(2)]
         dcol = [keep.tile([P, 4], F32, name="dcol%d" % h) for h in range(2)]
         drep = [keep.tile([P, 4 * P], F32, name="drep%d" % h) for h in range(2)]
-        dj = [dj_pool.tile([P, 4 * P], F32, name="dj%d" % h) for h in range(2)]
+        dj = [None, None]
 
         def d_rep(h):
             nc.scalar.activation(
@@ -129,18 +154,18 @@ def tile_structureawaregcn_kernel(tc, adjacency_matrix, node_features, W_gcn, W_
             )
             nc.scalar.sqrt(dcol[h][:], rec[h][:])
 
-        def t_dj(h, col_of):
+        def d_sq(h):
+            nc.scalar.sqrt(dcol[h][:], rec[h][:])
+
+        def t_dj(h):
             for k in range(4):
-                c = col_of[k]
-                nc.tensor.transpose(dj[h][:, k * P : (k + 1) * P], drep[h][:, c * P : (c + 1) * P], ident_f[:])
+                nc.tensor.transpose(dj[h][:, k * P : (k + 1) * P], dcol[h][:, k : k + 1].to_broadcast([P, P]), ident_f[:])
 
         ahat = [keep.tile([P, N_NODES], BF16, name="ahat%d" % m) for m in range(6)]
-        COL0 = [0, 2, 1, 3]
-        COL1 = [0, 1, 2, 3]
 
         def sc(m, g):
             in1 = dj[g][:].rearrange("i (t p) -> i t p", t=4) if g == 0 else dj[g][:].rearrange("i (p t) -> i t p", t=4)
-            c = COL0[m] if m < 4 else COL1[m - 4]
+            c = m % 4
             nc.vector.scalar_tensor_tensor(
                 out=ahat[m][:, g * 512 : (g + 1) * 512].rearrange("i (t p) -> i t p", t=4),
                 in0=a_rows[m][:, g * 512 : (g + 1) * 512].rearrange("i (p t) -> i t p", t=4),
@@ -157,45 +182,33 @@ def tile_structureawaregcn_kernel(tc, adjacency_matrix, node_features, W_gcn, W_
         pre = [keep.tile([P, D], F32, name="pre%d" % m) for m in range(6)]
         fin = [keep.tile([P, D], F32, name="fin%d" % m) for m in range(6)]
 
-        def at_one(bank, m, b):
-            nc.tensor.transpose(bank[:, b * P : (b + 1) * P], ahat[m][:, b * P : (b + 1) * P], ident_b[:])
+        def at_one(bk, m, b):
+            nc.tensor.transpose(bk[:, b * P : (b + 1) * P], ahat[m][:, b * P : (b + 1) * P], ident_b[:])
 
-        def at(m):
-            bank = tp_pool.tile([P, N_NODES], BF16, name="tpa", tag="tp")
-            for b in range(8):
-                at_one(bank, m, b)
-            return bank
-
-        def a_out(bank, m):
-            nc.scalar.copy(
-                out=agrp[m][:].rearrange("p (g i t) -> p g i t", g=2, t=4),
-                in_=bank[:].rearrange("p (g t i) -> p g i t", g=2, t=4),
-            )
+        def a_out(bk, m, eng):
+            dst_v = agrp[m][:].rearrange("p (g i t) -> p g i t", g=2, t=4)
+            src_v = bk[:].rearrange("p (g t i) -> p g i t", g=2, t=4)
+            if eng == "v":
+                nc.vector.tensor_copy(out=dst_v, in_=src_v)
+            else:
+                nc.scalar.copy(out=dst_v, in_=src_v)
 
         def q_a(m):
             nc.vector.quantize_mx(out=acodes[m][:].bitcast(FP8X4), scales=ascales[m][:], in_=agrp[m][:])
 
-        def sk(m, xt0, xt45, wsT, weave):
-            xt, col = (xt0, m * P) if m < 4 else (xt45, (m - 4) * P)
-            sacc = acc_pool.tile([P, D], F32, name="sacc", tag="acc")
-            bank = None
-            if weave is not None:
-                bank = tp_pool.tile([P, N_NODES], BF16, name="tpa", tag="tp")
-            for ci, (u, e) in enumerate(CHUNKS):
-                nc.tensor.matmul(sacc[:], lhsT=xt[:, u, col : col + P, e], rhs=wsT[:, u, :, e], start=(ci == 0), stop=(ci == 3))
-                if weave is not None:
-                    at_one(bank, weave, 2 * ci)
-                    at_one(bank, weave, 2 * ci + 1)
-            return sacc, bank
+        def sk_one(bk, m, ci):
+            xt = PAIRS["x0%d" % (m // 2)] if m < 4 else PAIRS["x45"]
+            col = (m % 2) * P
+            u, e = CHUNKS[ci]
+            nc.tensor.matmul(bk[:], lhsT=xt[:, u, col : col + P, e], rhs=wsT[:, u, :, e], start=(ci == 0), stop=(ci == 3))
 
-        def s_out(sacc, m):
-            nc.scalar.activation(out=skip_sb[m][:], in_=sacc[:], func=ACT.Copy, scale=0.5)
+        def s_out(bk, m):
+            nc.scalar.activation(out=skip_sb[m][:], in_=bk[:], func=ACT.Copy, scale=0.5)
 
-        def mx(m):
-            macc = acc_pool.tile([P, D], F32, name="macc", tag="acc")
+        def mx(bk, m):
             for g in range(2):
                 nc.tensor.matmul_mx(
-                    out=macc[:],
+                    out=bk[:],
                     lhsT=acodes[m][:, g * P : (g + 1) * P].bitcast(FP8X4),
                     lhsT_scale=ascales[m][:, g * P : (g + 1) * P],
                     rhs=hcodes[g][:].bitcast(FP8X4),
@@ -203,121 +216,280 @@ def tile_structureawaregcn_kernel(tc, adjacency_matrix, node_features, W_gcn, W_
                     start=(g == 0),
                     stop=(g == 1),
                 )
-            return macc
 
         out03 = out[0:512, :].rearrange("(p t) o -> p t o", t=4)
 
-        def ep(macc, m):
-            nc.vector.scalar_tensor_tensor(out=pre[m][:], in0=macc[:], scalar=0.5, in1=skip_sb[m][:], op0=ALU.mult, op1=ALU.add)
-            res = x0_sb[:, m * D : (m + 1) * D] if m < 4 else x45_sb[:, (m - 4) * D : (m - 3) * D]
+        def e1(bk, m):
+            nc.vector.scalar_tensor_tensor(out=pre[m][:], in0=bk[:], scalar=0.5, in1=skip_sb[m][:], op0=ALU.mult, op1=ALU.add)
+
+        def e2(m):
+            res = T["x0%d" % (m // 2)][:, (m % 2) * D : (m % 2 + 1) * D] if m < 4 else T["x45"][:, (m - 4) * D : (m - 3) * D]
             nc.vector.scalar_tensor_tensor(out=fin[m][:], in0=pre[m][:], scalar=0.0, in1=res, op0=ALU.max, op1=ALU.add)
+
+        def st(m):
             dst = out03[:, m, :] if m < 4 else out[P * m : P * (m + 1), :]
             nc.sync.dma_start(out=dst, in_=fin[m][:])
 
-        wgT_w = new_words("wgT", 4)
-        xt0_w = new_words("xt0", 4)
-        xt1_w = new_words("xt1", 4)
-        wsT_w = new_words("wsT", 4)
-        xt45_w = new_words("xt45", 2)
-        wgT, xt0, xt1, wsT, xt45 = pairs(wgT_w), pairs(xt0_w), pairs(xt1_w), pairs(wsT_w), pairs(xt45_w)
-        deg_v0 = keep.tile([P, 2], F32, name="deg_v0")
-        deg_s0 = keep.tile([P, 2], F32, name="deg_s0")
-        deg_v1 = keep.tile([P, 4], F32, name="deg_v1")
+        wsT_w = keep.tile([P, 8 * P], F32, name="wsT")
+        wsT = pairs(wsT_w)
+        WORDS = {}
+        PAIRS = {}
+        for key in ["wg0", "wg1", "x00", "x01", "x10", "x11", "x45"]:
+            WORDS[key] = keep.tile([P, 4 * P], F32, name="w_" + key)
+            PAIRS[key] = pairs(WORDS[key])
+        deg = [keep.tile([P, 4], F32, name="deg%d" % h) for h in range(2)]
 
-        c_w(t_w(wg_sb, 4, 0), wgT_w, 4, 0, "v")
-        c_w(t_w(wg_sb, 4, 1), wgT_w, 4, 1, "s")
-        c_w(t_w(x0_sb, 4, 0), xt0_w, 4, 0, "v")
-        c_w(t_w(x0_sb, 4, 1), xt0_w, 4, 1, "s")
-        b0 = h_mm(xt0, wgT, 0)
-        deg_v(0, deg_v0[:, 0:1])
-        deg_s(1, deg_s0[:, 0:1])
-        h_out(b0, 0, 0)
-        b1 = h_mm(xt0, wgT, 1)
-        deg_v(2, deg_v0[:, 1:2])
-        deg_s(3, deg_s0[:, 1:2])
-        h_out(b1, 0, 1)
-        b2 = h_mm(xt0, wgT, 2)
-        deg_v(4, deg_v1[:, 0:1])
-        deg_v(5, deg_v1[:, 1:2])
-        nc.vector.tensor_scalar_add(rec[0][:, 0:2], deg_v0[:], 1e-8)
-        nc.vector.tensor_scalar_add(rec[0][:, 2:4], deg_s0[:], 1e-8)
+        ld("wg0")
+        ld("x00")
+        ld("wg1")
+        ld("x01")
+        ld("a03_0")
+        ld("a03_1")
+        ld("x10")
+        ld("a4")
+        ld("a5")
+        ld("a6")
+        ld("a7")
+        ld("x11")
+        ld("ws0")
+        ld("ws1")
+        ld("x45")
+        k0 = bank(4, F32)
+        t_pair(T["wg0"], k0)
+        k1 = bank(5, F32)
+        t_pair(T["x00"], k1)
+        c_pair(k0, "wg0", "v")
+        k2 = bank(6, F32)
+        t_pair(T["wg1"], k2)
+        c_pair(k1, "x00", "s")
+        k3 = bank(7, F32)
+        t_pair(T["x01"], k3)
+        c_pair(k2, "wg1", "v")
+        k4 = bank(0, F32)
+        h_grp(k4, 0, 0, 0)
+        h_grp(k4, 0, 1, 0)
+        c_pair(k3, "x01", "s")
+        k5 = bank(1, F32)
+        h_grp(k5, 0, 0, 1)
+        h_grp(k5, 0, 1, 1)
+        deg_f(0, deg[0][:, 0:1])
+        k6 = bank(2, F32)
+        h_grp(k6, 0, 0, 2)
+        h_grp(k6, 0, 1, 2)
+        deg_f(1, deg[0][:, 1:2])
+        k7 = bank(3, F32)
+        h_grp(k7, 0, 0, 3)
+        h_grp(k7, 0, 1, 3)
+        deg_f(2, deg[0][:, 2:3])
+        h_grp(k4, 0, 2, 0)
+        h_grp(k4, 0, 3, 0)
+        deg_f(3, deg[0][:, 3:4])
+        nc.vector.tensor_scalar_add(rec[0][:], deg[0][:], 1e-8)
         nc.vector.reciprocal(rec[0][:], rec[0][:])
-        d_rep(0)
-        h_out(b2, 0, 2)
-        b3 = h_mm(xt0, wgT, 3)
-        deg_v(6, deg_v1[:, 2:3])
-        deg_v(7, deg_v1[:, 3:4])
-        nc.vector.tensor_scalar_add(rec[1][:], deg_v1[:], 1e-8)
+        h_grp(k5, 0, 2, 1)
+        h_grp(k5, 0, 3, 1)
+        d_sq(0)
+        deg_f(4, deg[1][:, 0:1])
+        h_out(k4, 0, 0, "s")
+        k8 = bank(4, F32)
+        t_pair(T["x10"], k8)
+        deg_f(5, deg[1][:, 1:2])
+        dj[0] = bank(5, F32)
+        t_dj(0)
+        h_out(k5, 0, 1, "s")
+        h_grp(k6, 0, 2, 2)
+        h_grp(k6, 0, 3, 2)
+        c_pair(k8, "x10", "s")
+        sc(0, 0)
+        h_grp(k7, 0, 2, 3)
+        h_grp(k7, 0, 3, 3)
+        h_out(k6, 0, 2, "s")
+        deg_f(6, deg[1][:, 2:3])
+        k9 = bank(0, F32)
+        h_grp(k9, 1, 0, 0)
+        h_grp(k9, 1, 1, 0)
+        sc(1, 0)
+        k10 = bank(1, F32)
+        h_grp(k10, 1, 0, 1)
+        h_grp(k10, 1, 1, 1)
+        deg_f(7, deg[1][:, 3:4])
+        nc.vector.tensor_scalar_add(rec[1][:], deg[1][:], 1e-8)
         nc.vector.reciprocal(rec[1][:], rec[1][:])
-        h_out(b3, 0, 3)
-        t_dj(0, COL0)
-        c_w(t_w(x1_sb, 4, 0), xt1_w, 4, 0, "s")
-        c_w(t_w(x1_sb, 4, 1), xt1_w, 4, 1, "s")
-        w0 = t_w(ws_sb, 4, 0)
-        w1 = t_w(ws_sb, 4, 1)
-        for m in range(4):
-            sc(m, 0)
-        d_rep(1)
-        c_w(w0, wsT_w, 4, 0, "s")
-        c_w(w1, wsT_w, 4, 1, "s")
-        b0 = h_mm(xt1, wgT, 0)
-        t_dj(1, COL1)
-        q_h(0)
-        h_out(b0, 1, 0)
-        b1 = h_mm(xt1, wgT, 1)
+        sc(2, 0)
+        d_sq(1)
+        h_out(k7, 0, 3, "s")
+        dj[1] = bank(6, F32)
+        t_dj(1)
+        sc(3, 0)
+        k11 = bank(7, F32)
+        t_pair(T["x11"], k11)
+        k12 = bank(2, F32)
+        h_grp(k12, 1, 0, 2)
+        h_grp(k12, 1, 1, 2)
         sc(0, 1)
-        h_out(b1, 1, 1)
-        t0 = at(0)
+        c_pair(k11, "x11", "s")
+        k13 = bank(3, F32)
+        h_grp(k13, 1, 0, 3)
+        h_grp(k13, 1, 1, 3)
         sc(1, 1)
-        a_out(t0, 0)
-        b2 = h_mm(xt1, wgT, 2)
-        h_out(b2, 1, 2)
-        t1 = at(1)
+        k14 = bank(4, F32)
+        t_pair(T["ws0"], k14)
+        q_h(0)
+        h_grp(k9, 1, 2, 0)
+        h_grp(k9, 1, 3, 0)
+        c_pair(k14, "ws0", "s")
         sc(2, 1)
-        a_out(t1, 1)
-        b3 = h_mm(xt1, wgT, 3)
-        h_out(b3, 1, 3)
-        t2 = at(2)
+        k15 = bank(7, F32)
+        t_pair(T["ws1"], k15)
+        h_out(k9, 1, 0, "s")
+        h_grp(k10, 1, 2, 1)
+        h_grp(k10, 1, 3, 1)
         sc(3, 1)
-        q_a(0)
-        a_out(t2, 2)
-        c_w(t_w(x45_sb, 2, 0), xt45_w, 2, 0, "s")
-        c_w(t_w(x45_sb, 2, 1), xt45_w, 2, 1, "s")
-        t3 = at(3)
+        c_pair(k15, "ws1", "s")
+        h_grp(k12, 1, 2, 2)
+        h_grp(k12, 1, 3, 2)
         sc(4, 0)
+        h_out(k10, 1, 1, "s")
+        h_grp(k13, 1, 2, 3)
+        h_grp(k13, 1, 3, 3)
         sc(4, 1)
-        q_a(1)
-        a_out(t3, 3)
-        q_h(1)
-        s0, t4 = sk(0, xt0, xt45, wsT, 4)
-        s_out(s0, 0)
+        h_out(k12, 1, 2, "s")
+        k16 = bank(4, F32)
+        t_pair(T["x45"], k16)
         sc(5, 0)
+        k17 = bank(7, BF16)
+        at_one(k17, 0, 0)
+        at_one(k17, 0, 1)
+        h_out(k13, 1, 3, "s")
+        at_one(k17, 0, 2)
+        at_one(k17, 0, 3)
+        at_one(k17, 0, 4)
+        at_one(k17, 0, 5)
+        at_one(k17, 0, 6)
         sc(5, 1)
+        at_one(k17, 0, 7)
+        k18 = bank(0, F32)
+        sk_one(k18, 0, 0)
+        c_pair(k16, "x45", "s")
+        k19 = bank(5, BF16)
+        at_one(k19, 1, 0)
+        at_one(k19, 1, 1)
+        at_one(k19, 1, 2)
+        sk_one(k18, 0, 1)
+        at_one(k19, 1, 3)
+        at_one(k19, 1, 4)
+        at_one(k19, 1, 5)
+        sk_one(k18, 0, 2)
+        a_out(k17, 0, "s")
+        at_one(k19, 1, 6)
+        at_one(k19, 1, 7)
+        k20 = bank(6, BF16)
+        at_one(k20, 2, 0)
+        sk_one(k18, 0, 3)
+        at_one(k20, 2, 1)
+        at_one(k20, 2, 2)
+        at_one(k20, 2, 3)
+        k21 = bank(1, F32)
+        sk_one(k21, 1, 0)
+        at_one(k20, 2, 4)
+        at_one(k20, 2, 5)
+        at_one(k20, 2, 6)
+        sk_one(k21, 1, 1)
+        a_out(k19, 1, "s")
+        at_one(k20, 2, 7)
+        k22 = bank(4, BF16)
+        at_one(k22, 3, 0)
+        at_one(k22, 3, 1)
+        q_a(0)
+        sk_one(k21, 1, 2)
+        at_one(k22, 3, 2)
+        at_one(k22, 3, 3)
+        q_h(1)
+        at_one(k22, 3, 4)
+        sk_one(k21, 1, 3)
+        at_one(k22, 3, 5)
+        at_one(k22, 3, 6)
+        at_one(k22, 3, 7)
+        s_out(k18, 0)
+        q_a(1)
+        k23 = bank(2, F32)
+        mx(k23, 0)
+        a_out(k20, 2, "s")
+        k24 = bank(3, F32)
+        sk_one(k24, 2, 0)
+        k25 = bank(7, BF16)
+        at_one(k25, 4, 0)
+        at_one(k25, 4, 1)
+        at_one(k25, 4, 2)
+        sk_one(k24, 2, 1)
+        at_one(k25, 4, 3)
+        at_one(k25, 4, 4)
+        at_one(k25, 4, 5)
+        sk_one(k24, 2, 2)
+        a_out(k22, 3, "s")
         q_a(2)
-        a_out(t4, 4)
-        s1, t5 = sk(1, xt0, xt45, wsT, 5)
-        s_out(s1, 1)
+        at_one(k25, 4, 6)
+        at_one(k25, 4, 7)
+        k26 = bank(5, BF16)
+        at_one(k26, 5, 0)
+        sk_one(k24, 2, 3)
+        e1(k23, 0)
+        at_one(k26, 5, 1)
+        at_one(k26, 5, 2)
+        at_one(k26, 5, 3)
+        k27 = bank(0, F32)
+        mx(k27, 1)
+        e2(0)
+        s_out(k21, 1)
+        k28 = bank(2, F32)
+        sk_one(k28, 3, 0)
+        at_one(k26, 5, 4)
+        at_one(k26, 5, 5)
+        at_one(k26, 5, 6)
+        sk_one(k28, 3, 1)
         q_a(3)
-        a_out(t5, 5)
-        m0 = mx(0)
-        m1 = mx(1)
-        ep(m0, 0)
-        s2, unused = sk(2, xt0, xt45, wsT, None)
-        s_out(s2, 2)
+        a_out(k25, 4, "s")
+        st(0)
+        at_one(k26, 5, 7)
+        sk_one(k28, 3, 2)
+        e1(k27, 1)
+        sk_one(k28, 3, 3)
+        k29 = bank(1, F32)
+        mx(k29, 2)
+        e2(1)
+        s_out(k24, 2)
+        k30 = bank(0, F32)
+        mx(k30, 3)
         q_a(4)
-        m2 = mx(2)
-        ep(m1, 1)
-        s3, unused = sk(3, xt0, xt45, wsT, None)
-        s_out(s3, 3)
+        st(1)
+        a_out(k26, 5, "s")
+        e1(k29, 2)
+        k31 = bank(3, F32)
+        sk_one(k31, 4, 0)
+        sk_one(k31, 4, 1)
+        e2(2)
+        sk_one(k31, 4, 2)
+        sk_one(k31, 4, 3)
+        s_out(k28, 3)
+        k32 = bank(1, F32)
+        mx(k32, 4)
         q_a(5)
-        m3 = mx(3)
-        ep(m2, 2)
-        s4, unused = sk(4, xt0, xt45, wsT, None)
-        s_out(s4, 4)
-        m4 = mx(4)
-        ep(m3, 3)
-        s5, unused = sk(5, xt0, xt45, wsT, None)
-        s_out(s5, 5)
-        m5 = mx(5)
-        ep(m4, 4)
-        ep(m5, 5)
+        st(2)
+        s_out(k31, 4)
+        e1(k30, 3)
+        k33 = bank(2, F32)
+        sk_one(k33, 5, 0)
+        sk_one(k33, 5, 1)
+        e2(3)
+        sk_one(k33, 5, 2)
+        sk_one(k33, 5, 3)
+        k34 = bank(3, F32)
+        mx(k34, 5)
+        e1(k32, 4)
+        st(3)
+        s_out(k33, 5)
+        e2(4)
+        e1(k34, 5)
+        st(4)
+        e2(5)
+        st(5)

@@ -78,17 +78,16 @@ def tile_structureawaregcn_kernel(tc, adjacency_matrix, node_features, W_gcn, W_
         def pairs(dst):
             return dst[:].bitcast(BF16).rearrange("q (u n e) -> q u n e", u=2, e=2)
 
-        def t_pair(src, bk):
+        def t_one(src, bk, k):
             words = src[:].bitcast(F32)
-            for u in range(2):
-                for b in range(2):
-                    k = 2 * u + b
-                    nc.tensor.transpose(bk[:, k * P : (k + 1) * P], words[:, b * 256 + u * P : b * 256 + (u + 1) * P], ident_f[:])
+            u, b = k // 2, k % 2
+            nc.tensor.transpose(bk[:, k * P : (k + 1) * P], words[:, b * 256 + u * P : b * 256 + (u + 1) * P], ident_f[:])
 
         def c_pair(bk, key, eng):
-            if key == "ws0" or key == "ws1":
-                b0 = 0 if key == "ws0" else 2
-                dst_v = wsT_w[:].rearrange("q (u n) -> q u n", u=2)[:, :, b0 * P : (b0 + 2) * P]
+            if key[0] == "w":
+                b0 = 0 if key[2] == "0" else 2
+                whole = wsT_w if key[1] == "s" else wgT_w
+                dst_v = whole[:].rearrange("q (u n) -> q u n", u=2)[:, :, b0 * P : (b0 + 2) * P]
                 src_v = bk[:].rearrange("q (u n) -> q u n", u=2)
             else:
                 dst_v = WORDS[key][:]
@@ -102,25 +101,29 @@ def tile_structureawaregcn_kernel(tc, adjacency_matrix, node_features, W_gcn, W_
         hcodes = [keep.tile([P, D], U32, name="hcodes%d" % g, align_bytes=64) for g in range(2)]
         hscales = [keep.tile([P, D], U8, name="hscales%d" % g, align_bytes=64) for g in range(2)]
 
-        def h_grp(bk, g, t, oc):
-            xt = PAIRS["x%d%d" % (g, t // 2)]
-            wt = PAIRS["wg%d" % (oc // 2)]
-            for ci, (u, e) in enumerate(CHUNKS):
-                nc.tensor.matmul(
-                    bk[:, t * P : (t + 1) * P],
-                    lhsT=xt[:, u, (t % 2) * P : (t % 2 + 1) * P, e],
-                    rhs=wt[:, u, (oc % 2) * P : (oc % 2 + 1) * P, e],
-                    start=(ci == 0),
-                    stop=(ci == 3),
-                )
+        hsb = [keep.tile([P, 4 * D], BF16, name="hsb%d" % g) for g in range(2)]
 
-        def h_out(bk, g, oc, eng):
-            dst_v = hgrp[g][:, oc * 512 : (oc + 1) * 512].rearrange("p (o t) -> p o t", t=4)
-            src_v = bk[:].rearrange("p (t o) -> p o t", t=4)
+        def h_one(bk, g, t, ci):
+            xt = PAIRS["x%d%d" % (g, t // 2)]
+            u, e = CHUNKS[ci]
+            nc.tensor.matmul(bk[:], lhsT=xt[:, u, (t % 2) * P : (t % 2 + 1) * P, e], rhs=wgT[:, u, :, e], start=(ci == 0), stop=(ci == 3))
+
+        def h_out(bk, g, t, eng):
+            dst_v = hsb[g][:, t * D : (t + 1) * D]
+            if eng == "v":
+                nc.vector.tensor_copy(out=dst_v, in_=bk[:])
+            else:
+                nc.scalar.copy(out=dst_v, in_=bk[:])
+
+        def rg(g, half, eng):
+            dst_v = hgrp[g][:, half * 1024 : (half + 1) * 1024].rearrange("p (c i t) -> p c t i", i=4, t=4)
+            src_v = hsb[g][:].rearrange("p (t o) -> p t o", t=4)[:, :, half * 256 : (half + 1) * 256].rearrange("p t (c i) -> p c t i", i=4)
             if eng == "v":
                 nc.vector.tensor_copy(out=dst_v, in_=src_v)
-            else:
+            elif eng == "s":
                 nc.scalar.copy(out=dst_v, in_=src_v)
+            else:
+                nc.gpsimd.tensor_scalar(out=dst_v, in0=src_v, scalar1=1.0, scalar2=0.0, op0=ALU.mult, op1=ALU.add)
 
         def q_h(g):
             nc.vector.quantize_mx(out=hcodes[g][:].bitcast(FP8X4), scales=hscales[g][:], in_=hgrp[g][:])
@@ -157,9 +160,8 @@ def tile_structureawaregcn_kernel(tc, adjacency_matrix, node_features, W_gcn, W_
         def d_sq(h):
             nc.scalar.sqrt(dcol[h][:], rec[h][:])
 
-        def t_dj(h):
-            for k in range(4):
-                nc.tensor.transpose(dj[h][:, k * P : (k + 1) * P], dcol[h][:, k : k + 1].to_broadcast([P, P]), ident_f[:])
+        def t_dj_one(h, k):
+            nc.tensor.transpose(dj[h][:, k * P : (k + 1) * P], dcol[h][:, k : k + 1].to_broadcast([P, P]), ident_f[:])
 
         ahat = [keep.tile([P, N_NODES], BF16, name="ahat%d" % m) for m in range(6)]
 
@@ -226,15 +228,22 @@ def tile_structureawaregcn_kernel(tc, adjacency_matrix, node_features, W_gcn, W_
             res = T["x0%d" % (m // 2)][:, (m % 2) * D : (m % 2 + 1) * D] if m < 4 else T["x45"][:, (m - 4) * D : (m - 3) * D]
             nc.vector.scalar_tensor_tensor(out=fin[m][:], in0=pre[m][:], scalar=0.0, in1=res, op0=ALU.max, op1=ALU.add)
 
+        def e2g(m):
+            res = T["x0%d" % (m // 2)][:, (m % 2) * D : (m % 2 + 1) * D] if m < 4 else T["x45"][:, (m - 4) * D : (m - 3) * D]
+            nc.gpsimd.tensor_scalar(out=pre[m][:], in0=pre[m][:], scalar1=0.0, scalar2=0.0, op0=ALU.max, op1=ALU.add)
+            nc.gpsimd.tensor_tensor(out=fin[m][:], in0=pre[m][:], in1=res, op=ALU.add)
+
         def st(m):
             dst = out03[:, m, :] if m < 4 else out[P * m : P * (m + 1), :]
             nc.sync.dma_start(out=dst, in_=fin[m][:])
 
         wsT_w = keep.tile([P, 8 * P], F32, name="wsT")
         wsT = pairs(wsT_w)
+        wgT_w = keep.tile([P, 8 * P], F32, name="wgT")
+        wgT = pairs(wgT_w)
         WORDS = {}
         PAIRS = {}
-        for key in ["wg0", "wg1", "x00", "x01", "x10", "x11", "x45"]:
+        for key in ["x00", "x01", "x10", "x11", "x45"]:
             WORDS[key] = keep.tile([P, 4 * P], F32, name="w_" + key)
             PAIRS[key] = pairs(WORDS[key])
         deg = [keep.tile([P, 4], F32, name="deg%d" % h) for h in range(2)]
@@ -255,240 +264,277 @@ def tile_structureawaregcn_kernel(tc, adjacency_matrix, node_features, W_gcn, W_
         ld("ws1")
         ld("x45")
         k0 = bank(4, F32)
-        t_pair(T["wg0"], k0)
+        t_one(T["x00"], k0, 0)
         k1 = bank(5, F32)
-        t_pair(T["x00"], k1)
-        c_pair(k0, "wg0", "v")
+        t_one(T["wg0"], k1, 0)
+        t_one(T["wg0"], k1, 1)
         k2 = bank(6, F32)
-        t_pair(T["wg1"], k2)
-        c_pair(k1, "x00", "s")
+        t_one(T["wg1"], k2, 0)
+        t_one(T["wg1"], k2, 1)
+        t_one(T["wg1"], k2, 2)
+        t_one(T["x00"], k0, 1)
+        t_one(T["wg1"], k2, 3)
+        t_one(T["x00"], k0, 2)
+        t_one(T["wg0"], k1, 2)
+        t_one(T["wg0"], k1, 3)
         k3 = bank(7, F32)
-        t_pair(T["x01"], k3)
+        t_one(T["x01"], k3, 0)
         c_pair(k2, "wg1", "v")
-        k4 = bank(0, F32)
-        h_grp(k4, 0, 0, 0)
-        h_grp(k4, 0, 1, 0)
+        t_one(T["x00"], k0, 3)
+        t_one(T["x01"], k3, 1)
+        t_one(T["x01"], k3, 2)
+        t_one(T["x01"], k3, 3)
+        c_pair(k0, "x00", "s")
+        c_pair(k1, "wg0", "v")
         c_pair(k3, "x01", "s")
-        k5 = bank(1, F32)
-        h_grp(k5, 0, 0, 1)
-        h_grp(k5, 0, 1, 1)
         deg_f(0, deg[0][:, 0:1])
-        k6 = bank(2, F32)
-        h_grp(k6, 0, 0, 2)
-        h_grp(k6, 0, 1, 2)
-        deg_f(1, deg[0][:, 1:2])
-        k7 = bank(3, F32)
-        h_grp(k7, 0, 0, 3)
-        h_grp(k7, 0, 1, 3)
-        deg_f(2, deg[0][:, 2:3])
-        h_grp(k4, 0, 2, 0)
-        h_grp(k4, 0, 3, 0)
+        k4 = bank(0, F32)
+        h_one(k4, 0, 1, 0)
+        h_one(k4, 0, 1, 1)
+        h_one(k4, 0, 1, 2)
+        k5 = bank(1, F32)
+        h_one(k5, 0, 0, 0)
         deg_f(3, deg[0][:, 3:4])
+        k6 = bank(2, F32)
+        h_one(k6, 0, 2, 0)
+        deg_f(1, deg[0][:, 1:2])
+        k7 = bank(6, F32)
+        t_one(T["x10"], k7, 0)
+        k8 = bank(3, F32)
+        h_one(k8, 0, 3, 0)
+        deg_f(2, deg[0][:, 2:3])
+        h_one(k6, 0, 2, 1)
+        t_one(T["x10"], k7, 1)
+        h_one(k6, 0, 2, 2)
         nc.vector.tensor_scalar_add(rec[0][:], deg[0][:], 1e-8)
         nc.vector.reciprocal(rec[0][:], rec[0][:])
-        h_grp(k5, 0, 2, 1)
-        h_grp(k5, 0, 3, 1)
-        d_sq(0)
         deg_f(4, deg[1][:, 0:1])
-        h_out(k4, 0, 0, "s")
-        k8 = bank(4, F32)
-        t_pair(T["x10"], k8)
+        t_one(T["x10"], k7, 2)
+        t_one(T["x10"], k7, 3)
+        h_one(k4, 0, 1, 3)
+        d_sq(0)
+        h_one(k8, 0, 3, 1)
+        c_pair(k7, "x10", "s")
         deg_f(5, deg[1][:, 1:2])
-        dj[0] = bank(5, F32)
-        t_dj(0)
-        h_out(k5, 0, 1, "s")
-        h_grp(k6, 0, 2, 2)
-        h_grp(k6, 0, 3, 2)
-        c_pair(k8, "x10", "s")
-        sc(0, 0)
-        h_grp(k7, 0, 2, 3)
-        h_grp(k7, 0, 3, 3)
-        h_out(k6, 0, 2, "s")
+        dj[0] = bank(4, F32)
+        t_dj_one(0, 0)
+        t_dj_one(0, 1)
+        h_one(k6, 0, 2, 3)
+        h_one(k5, 0, 0, 1)
         deg_f(6, deg[1][:, 2:3])
-        k9 = bank(0, F32)
-        h_grp(k9, 1, 0, 0)
-        h_grp(k9, 1, 1, 0)
-        sc(1, 0)
-        k10 = bank(1, F32)
-        h_grp(k10, 1, 0, 1)
-        h_grp(k10, 1, 1, 1)
+        t_dj_one(0, 2)
+        t_dj_one(0, 3)
+        h_one(k8, 0, 3, 2)
+        h_out(k6, 0, 2, "s")
+        h_one(k8, 0, 3, 3)
         deg_f(7, deg[1][:, 3:4])
+        h_one(k5, 0, 0, 2)
+        h_out(k4, 0, 1, "s")
         nc.vector.tensor_scalar_add(rec[1][:], deg[1][:], 1e-8)
         nc.vector.reciprocal(rec[1][:], rec[1][:])
-        sc(2, 0)
+        sc(1, 0)
+        k9 = bank(5, F32)
+        t_one(T["x11"], k9, 0)
+        h_one(k5, 0, 0, 3)
         d_sq(1)
-        h_out(k7, 0, 3, "s")
-        dj[1] = bank(6, F32)
-        t_dj(1)
+        t_one(T["x11"], k9, 1)
+        t_one(T["x11"], k9, 2)
+        k10 = bank(2, F32)
+        h_one(k10, 1, 0, 0)
+        t_one(T["x11"], k9, 3)
+        sc(2, 0)
+        h_one(k10, 1, 0, 1)
+        h_out(k5, 0, 0, "s")
+        dj[1] = bank(7, F32)
+        t_dj_one(1, 0)
+        h_one(k10, 1, 0, 2)
+        c_pair(k9, "x11", "s")
+        t_dj_one(1, 1)
+        k11 = bank(6, F32)
+        t_one(T["ws1"], k11, 0)
         sc(3, 0)
-        k11 = bank(7, F32)
-        t_pair(T["x11"], k11)
-        k12 = bank(2, F32)
-        h_grp(k12, 1, 0, 2)
-        h_grp(k12, 1, 1, 2)
-        sc(0, 1)
-        c_pair(k11, "x11", "s")
-        k13 = bank(3, F32)
-        h_grp(k13, 1, 0, 3)
-        h_grp(k13, 1, 1, 3)
-        sc(1, 1)
-        k14 = bank(4, F32)
-        t_pair(T["ws0"], k14)
-        q_h(0)
-        h_grp(k9, 1, 2, 0)
-        h_grp(k9, 1, 3, 0)
-        c_pair(k14, "ws0", "s")
-        sc(2, 1)
-        k15 = bank(7, F32)
-        t_pair(T["ws1"], k15)
-        h_out(k9, 1, 0, "s")
-        h_grp(k10, 1, 2, 1)
-        h_grp(k10, 1, 3, 1)
-        sc(3, 1)
-        c_pair(k15, "ws1", "s")
-        h_grp(k12, 1, 2, 2)
-        h_grp(k12, 1, 3, 2)
-        sc(4, 0)
-        h_out(k10, 1, 1, "s")
-        h_grp(k13, 1, 2, 3)
-        h_grp(k13, 1, 3, 3)
-        sc(4, 1)
-        h_out(k12, 1, 2, "s")
-        k16 = bank(4, F32)
-        t_pair(T["x45"], k16)
+        k12 = bank(0, F32)
+        h_one(k12, 1, 1, 0)
+        t_one(T["ws1"], k11, 1)
+        h_one(k12, 1, 1, 1)
+        h_out(k8, 0, 3, "s")
+        t_one(T["ws1"], k11, 2)
+        t_one(T["ws1"], k11, 3)
+        h_one(k12, 1, 1, 2)
         sc(5, 0)
-        k17 = bank(7, BF16)
-        at_one(k17, 0, 0)
-        at_one(k17, 0, 1)
-        h_out(k13, 1, 3, "s")
-        at_one(k17, 0, 2)
-        at_one(k17, 0, 3)
-        at_one(k17, 0, 4)
-        at_one(k17, 0, 5)
-        at_one(k17, 0, 6)
+        k13 = bank(5, F32)
+        t_one(T["ws0"], k13, 0)
+        t_one(T["ws0"], k13, 1)
+        h_one(k10, 1, 0, 3)
+        c_pair(k11, "ws1", "s")
+        t_one(T["ws0"], k13, 2)
+        t_one(T["ws0"], k13, 3)
+        k14 = bank(1, F32)
+        h_one(k14, 1, 2, 0)
+        rg(0, 1, "g")
+        sc(4, 0)
+        h_one(k14, 1, 2, 1)
+        h_out(k10, 1, 0, "s")
+        t_dj_one(1, 2)
+        t_dj_one(1, 3)
+        h_one(k14, 1, 2, 2)
+        sc(0, 0)
+        h_one(k14, 1, 2, 3)
+        c_pair(k13, "ws0", "s")
+        h_one(k12, 1, 1, 3)
+        sc(0, 1)
+        k15 = bank(6, BF16)
+        at_one(k15, 0, 0)
+        k16 = bank(4, BF16)
+        at_one(k16, 1, 0)
+        at_one(k16, 1, 1)
+        at_one(k15, 0, 1)
+        rg(0, 0, "g")
+        at_one(k16, 1, 2)
+        h_out(k14, 1, 2, "s")
+        at_one(k15, 0, 2)
+        at_one(k15, 0, 3)
+        k17 = bank(3, F32)
+        h_one(k17, 1, 3, 0)
+        sc(1, 1)
+        at_one(k15, 0, 4)
+        k18 = bank(5, F32)
+        t_one(T["x45"], k18, 0)
+        at_one(k15, 0, 5)
+        at_one(k15, 0, 6)
+        h_out(k12, 1, 1, "s")
+        at_one(k15, 0, 7)
+        h_one(k17, 1, 3, 1)
+        sc(3, 1)
+        at_one(k16, 1, 3)
+        t_one(T["x45"], k18, 1)
+        h_one(k17, 1, 3, 2)
+        a_out(k15, 0, "s")
+        k19 = bank(2, F32)
+        sk_one(k19, 0, 0)
         sc(5, 1)
-        at_one(k17, 0, 7)
-        k18 = bank(0, F32)
-        sk_one(k18, 0, 0)
-        c_pair(k16, "x45", "s")
-        k19 = bank(5, BF16)
-        at_one(k19, 1, 0)
-        at_one(k19, 1, 1)
-        at_one(k19, 1, 2)
-        sk_one(k18, 0, 1)
-        at_one(k19, 1, 3)
-        at_one(k19, 1, 4)
-        at_one(k19, 1, 5)
-        sk_one(k18, 0, 2)
-        a_out(k17, 0, "s")
-        at_one(k19, 1, 6)
-        at_one(k19, 1, 7)
-        k20 = bank(6, BF16)
-        at_one(k20, 2, 0)
-        sk_one(k18, 0, 3)
-        at_one(k20, 2, 1)
-        at_one(k20, 2, 2)
-        at_one(k20, 2, 3)
-        k21 = bank(1, F32)
-        sk_one(k21, 1, 0)
-        at_one(k20, 2, 4)
-        at_one(k20, 2, 5)
-        at_one(k20, 2, 6)
-        sk_one(k21, 1, 1)
-        a_out(k19, 1, "s")
-        at_one(k20, 2, 7)
-        k22 = bank(4, BF16)
-        at_one(k22, 3, 0)
-        at_one(k22, 3, 1)
+        t_one(T["x45"], k18, 2)
+        t_one(T["x45"], k18, 3)
+        k20 = bank(1, F32)
+        sk_one(k20, 2, 0)
+        h_one(k17, 1, 3, 3)
+        sk_one(k20, 2, 1)
+        sc(4, 1)
+        c_pair(k18, "x45", "s")
+        k21 = bank(6, BF16)
+        at_one(k21, 3, 0)
+        sk_one(k20, 2, 2)
+        k22 = bank(0, F32)
+        sk_one(k22, 1, 0)
+        sc(2, 1)
+        h_out(k17, 1, 3, "s")
+        k23 = bank(5, BF16)
+        at_one(k23, 4, 0)
+        at_one(k21, 3, 1)
+        at_one(k21, 3, 2)
+        at_one(k21, 3, 3)
+        at_one(k16, 1, 4)
+        sk_one(k22, 1, 1)
+        q_h(0)
+        rg(1, 1, "s")
+        at_one(k16, 1, 5)
+        at_one(k16, 1, 6)
+        at_one(k23, 4, 1)
+        k24 = bank(7, BF16)
+        at_one(k24, 2, 0)
+        at_one(k23, 4, 2)
+        at_one(k16, 1, 7)
+        sk_one(k19, 0, 1)
         q_a(0)
-        sk_one(k21, 1, 2)
-        at_one(k22, 3, 2)
-        at_one(k22, 3, 3)
+        at_one(k24, 2, 1)
+        at_one(k24, 2, 2)
+        at_one(k21, 3, 4)
+        at_one(k24, 2, 3)
+        at_one(k23, 4, 3)
+        at_one(k23, 4, 4)
+        sk_one(k19, 0, 2)
+        rg(1, 0, "v")
+        at_one(k21, 3, 5)
+        sk_one(k19, 0, 3)
+        a_out(k16, 1, "s")
+        at_one(k24, 2, 4)
+        sk_one(k22, 1, 2)
         q_h(1)
-        at_one(k22, 3, 4)
-        sk_one(k21, 1, 3)
-        at_one(k22, 3, 5)
-        at_one(k22, 3, 6)
-        at_one(k22, 3, 7)
-        s_out(k18, 0)
+        at_one(k24, 2, 5)
+        at_one(k21, 3, 6)
+        sk_one(k20, 2, 3)
+        at_one(k23, 4, 5)
+        sk_one(k22, 1, 3)
+        s_out(k19, 0)
         q_a(1)
-        k23 = bank(2, F32)
-        mx(k23, 0)
-        a_out(k20, 2, "s")
-        k24 = bank(3, F32)
-        sk_one(k24, 2, 0)
-        k25 = bank(7, BF16)
-        at_one(k25, 4, 0)
-        at_one(k25, 4, 1)
-        at_one(k25, 4, 2)
-        sk_one(k24, 2, 1)
-        at_one(k25, 4, 3)
-        at_one(k25, 4, 4)
-        at_one(k25, 4, 5)
-        sk_one(k24, 2, 2)
-        a_out(k22, 3, "s")
-        q_a(2)
-        at_one(k25, 4, 6)
-        at_one(k25, 4, 7)
-        k26 = bank(5, BF16)
-        at_one(k26, 5, 0)
-        sk_one(k24, 2, 3)
-        e1(k23, 0)
-        at_one(k26, 5, 1)
-        at_one(k26, 5, 2)
-        at_one(k26, 5, 3)
-        k27 = bank(0, F32)
-        mx(k27, 1)
-        e2(0)
-        s_out(k21, 1)
-        k28 = bank(2, F32)
-        sk_one(k28, 3, 0)
-        at_one(k26, 5, 4)
-        at_one(k26, 5, 5)
-        at_one(k26, 5, 6)
-        sk_one(k28, 3, 1)
-        q_a(3)
-        a_out(k25, 4, "s")
-        st(0)
-        at_one(k26, 5, 7)
-        sk_one(k28, 3, 2)
-        e1(k27, 1)
-        sk_one(k28, 3, 3)
+        k25 = bank(3, F32)
+        mx(k25, 0)
+        s_out(k22, 1)
+        k26 = bank(2, F32)
+        sk_one(k26, 3, 0)
+        at_one(k24, 2, 6)
+        at_one(k21, 3, 7)
+        at_one(k24, 2, 7)
+        e1(k25, 0)
+        k27 = bank(4, BF16)
+        at_one(k27, 5, 0)
+        s_out(k20, 2)
+        sk_one(k26, 3, 1)
+        at_one(k27, 5, 1)
+        at_one(k27, 5, 2)
+        sk_one(k26, 3, 2)
+        a_out(k21, 3, "s")
+        a_out(k24, 2, "v")
+        at_one(k27, 5, 3)
+        at_one(k27, 5, 4)
+        k28 = bank(0, F32)
+        mx(k28, 1)
+        e2g(0)
+        sk_one(k26, 3, 3)
+        at_one(k27, 5, 5)
+        at_one(k23, 4, 6)
         k29 = bank(1, F32)
-        mx(k29, 2)
-        e2(1)
-        s_out(k24, 2)
-        k30 = bank(0, F32)
-        mx(k30, 3)
+        sk_one(k29, 5, 0)
+        q_a(2)
+        at_one(k23, 4, 7)
+        s_out(k26, 3)
+        at_one(k27, 5, 6)
+        at_one(k27, 5, 7)
+        k30 = bank(3, F32)
+        sk_one(k30, 4, 0)
+        e1(k28, 1)
+        a_out(k23, 4, "s")
+        q_a(3)
+        k31 = bank(2, F32)
+        mx(k31, 2)
+        e2g(1)
+        st(0)
+        sk_one(k29, 5, 1)
+        k32 = bank(0, F32)
+        mx(k32, 3)
+        e1(k31, 2)
+        a_out(k27, 5, "s")
+        sk_one(k30, 4, 1)
         q_a(4)
+        sk_one(k30, 4, 2)
+        e1(k32, 3)
+        sk_one(k30, 4, 3)
+        e2g(2)
+        sk_one(k29, 5, 2)
         st(1)
-        a_out(k26, 5, "s")
-        e1(k29, 2)
-        k31 = bank(3, F32)
-        sk_one(k31, 4, 0)
-        sk_one(k31, 4, 1)
-        e2(2)
-        sk_one(k31, 4, 2)
-        sk_one(k31, 4, 3)
-        s_out(k28, 3)
-        k32 = bank(1, F32)
-        mx(k32, 4)
         q_a(5)
-        st(2)
-        s_out(k31, 4)
-        e1(k30, 3)
         k33 = bank(2, F32)
-        sk_one(k33, 5, 0)
-        sk_one(k33, 5, 1)
+        mx(k33, 4)
+        s_out(k30, 4)
         e2(3)
-        sk_one(k33, 5, 2)
-        sk_one(k33, 5, 3)
-        k34 = bank(3, F32)
+        sk_one(k29, 5, 3)
+        k34 = bank(0, F32)
         mx(k34, 5)
-        e1(k32, 4)
-        st(3)
-        s_out(k33, 5)
+        e1(k33, 4)
+        s_out(k29, 5)
         e2(4)
+        st(2)
+        st(3)
         e1(k34, 5)
         st(4)
         e2(5)

@@ -39,6 +39,13 @@ def tile_structureawaregcn_kernel(tc, adjacency_matrix, node_features, W_gcn, W_
         nc.vector.memset(warm[:], 1.0)
         nc.scalar.sqrt(warm[:], warm[:])
 
+        zeros_f = keep.tile([P, P], F32, name="zeros_f")
+        nc.vector.memset(zeros_f[:], 0.0)
+
+        def warm_up(bk, n):
+            for r in range(n):
+                nc.tensor.matmul(bk[:, 0:P], lhsT=zeros_f[:], rhs=zeros_f[:], start=True, stop=True)
+
         x_lo = node_features[0:512, :].rearrange("(p t) c -> p t c", t=4)
         x_hi = node_features[512:1024, :].rearrange("(p t) c -> p t c", t=4)
         a_lo = adjacency_matrix[0:512, :].rearrange("(p t) j -> p t j", t=4)
@@ -78,16 +85,17 @@ def tile_structureawaregcn_kernel(tc, adjacency_matrix, node_features, W_gcn, W_
         def pairs(dst):
             return dst[:].bitcast(BF16).rearrange("q (u n e) -> q u n e", u=2, e=2)
 
-        def t_one(src, bk, k):
+        def t_pair(src, bk):
             words = src[:].bitcast(F32)
-            u, b = k // 2, k % 2
-            nc.tensor.transpose(bk[:, k * P : (k + 1) * P], words[:, b * 256 + u * P : b * 256 + (u + 1) * P], ident_f[:])
+            for u in range(2):
+                for b in range(2):
+                    k = 2 * u + b
+                    nc.tensor.transpose(bk[:, k * P : (k + 1) * P], words[:, b * 256 + u * P : b * 256 + (u + 1) * P], ident_f[:])
 
         def c_pair(bk, key, eng):
-            if key[0] == "w":
-                b0 = 0 if key[2] == "0" else 2
-                whole = wsT_w if key[1] == "s" else wgT_w
-                dst_v = whole[:].rearrange("q (u n) -> q u n", u=2)[:, :, b0 * P : (b0 + 2) * P]
+            if key == "ws0" or key == "ws1":
+                b0 = 0 if key == "ws0" else 2
+                dst_v = wsT_w[:].rearrange("q (u n) -> q u n", u=2)[:, :, b0 * P : (b0 + 2) * P]
                 src_v = bk[:].rearrange("q (u n) -> q u n", u=2)
             else:
                 dst_v = WORDS[key][:]
@@ -101,29 +109,25 @@ def tile_structureawaregcn_kernel(tc, adjacency_matrix, node_features, W_gcn, W_
         hcodes = [keep.tile([P, D], U32, name="hcodes%d" % g, align_bytes=64) for g in range(2)]
         hscales = [keep.tile([P, D], U8, name="hscales%d" % g, align_bytes=64) for g in range(2)]
 
-        hsb = [keep.tile([P, 4 * D], BF16, name="hsb%d" % g) for g in range(2)]
-
-        def h_one(bk, g, t, ci):
+        def h_grp(bk, g, t, oc):
             xt = PAIRS["x%d%d" % (g, t // 2)]
-            u, e = CHUNKS[ci]
-            nc.tensor.matmul(bk[:], lhsT=xt[:, u, (t % 2) * P : (t % 2 + 1) * P, e], rhs=wgT[:, u, :, e], start=(ci == 0), stop=(ci == 3))
+            wt = PAIRS["wg%d" % (oc // 2)]
+            for ci, (u, e) in enumerate(CHUNKS):
+                nc.tensor.matmul(
+                    bk[:, t * P : (t + 1) * P],
+                    lhsT=xt[:, u, (t % 2) * P : (t % 2 + 1) * P, e],
+                    rhs=wt[:, u, (oc % 2) * P : (oc % 2 + 1) * P, e],
+                    start=(ci == 0),
+                    stop=(ci == 3),
+                )
 
-        def h_out(bk, g, t, eng):
-            dst_v = hsb[g][:, t * D : (t + 1) * D]
-            if eng == "v":
-                nc.vector.tensor_copy(out=dst_v, in_=bk[:])
-            else:
-                nc.scalar.copy(out=dst_v, in_=bk[:])
-
-        def rg(g, half, eng):
-            dst_v = hgrp[g][:, half * 1024 : (half + 1) * 1024].rearrange("p (c i t) -> p c t i", i=4, t=4)
-            src_v = hsb[g][:].rearrange("p (t o) -> p t o", t=4)[:, :, half * 256 : (half + 1) * 256].rearrange("p t (c i) -> p c t i", i=4)
+        def h_out(bk, g, oc, eng):
+            dst_v = hgrp[g][:, oc * 512 : (oc + 1) * 512].rearrange("p (o t) -> p o t", t=4)
+            src_v = bk[:].rearrange("p (t o) -> p o t", t=4)
             if eng == "v":
                 nc.vector.tensor_copy(out=dst_v, in_=src_v)
-            elif eng == "s":
-                nc.scalar.copy(out=dst_v, in_=src_v)
             else:
-                nc.gpsimd.tensor_scalar(out=dst_v, in0=src_v, scalar1=1.0, scalar2=0.0, op0=ALU.mult, op1=ALU.add)
+                nc.scalar.copy(out=dst_v, in_=src_v)
 
         def q_h(g):
             nc.vector.quantize_mx(out=hcodes[g][:].bitcast(FP8X4), scales=hscales[g][:], in_=hgrp[g][:])
@@ -160,8 +164,9 @@ def tile_structureawaregcn_kernel(tc, adjacency_matrix, node_features, W_gcn, W_
         def d_sq(h):
             nc.scalar.sqrt(dcol[h][:], rec[h][:])
 
-        def t_dj_one(h, k):
-            nc.tensor.transpose(dj[h][:, k * P : (k + 1) * P], dcol[h][:, k : k + 1].to_broadcast([P, P]), ident_f[:])
+        def t_dj(h):
+            for k in range(4):
+                nc.tensor.transpose(dj[h][:, k * P : (k + 1) * P], dcol[h][:, k : k + 1].to_broadcast([P, P]), ident_f[:])
 
         ahat = [keep.tile([P, N_NODES], BF16, name="ahat%d" % m) for m in range(6)]
 
@@ -228,22 +233,15 @@ def tile_structureawaregcn_kernel(tc, adjacency_matrix, node_features, W_gcn, W_
             res = T["x0%d" % (m // 2)][:, (m % 2) * D : (m % 2 + 1) * D] if m < 4 else T["x45"][:, (m - 4) * D : (m - 3) * D]
             nc.vector.scalar_tensor_tensor(out=fin[m][:], in0=pre[m][:], scalar=0.0, in1=res, op0=ALU.max, op1=ALU.add)
 
-        def e2g(m):
-            res = T["x0%d" % (m // 2)][:, (m % 2) * D : (m % 2 + 1) * D] if m < 4 else T["x45"][:, (m - 4) * D : (m - 3) * D]
-            nc.gpsimd.tensor_scalar(out=pre[m][:], in0=pre[m][:], scalar1=0.0, scalar2=0.0, op0=ALU.max, op1=ALU.add)
-            nc.gpsimd.tensor_tensor(out=fin[m][:], in0=pre[m][:], in1=res, op=ALU.add)
-
         def st(m):
             dst = out03[:, m, :] if m < 4 else out[P * m : P * (m + 1), :]
             nc.sync.dma_start(out=dst, in_=fin[m][:])
 
         wsT_w = keep.tile([P, 8 * P], F32, name="wsT")
         wsT = pairs(wsT_w)
-        wgT_w = keep.tile([P, 8 * P], F32, name="wgT")
-        wgT = pairs(wgT_w)
         WORDS = {}
         PAIRS = {}
-        for key in ["x00", "x01", "x10", "x11", "x45"]:
+        for key in ["wg0", "wg1", "x00", "x01", "x10", "x11", "x45"]:
             WORDS[key] = keep.tile([P, 4 * P], F32, name="w_" + key)
             PAIRS[key] = pairs(WORDS[key])
         deg = [keep.tile([P, 4], F32, name="deg%d" % h) for h in range(2)]
@@ -263,278 +261,245 @@ def tile_structureawaregcn_kernel(tc, adjacency_matrix, node_features, W_gcn, W_
         ld("ws0")
         ld("ws1")
         ld("x45")
+        kw = bank(7, F32)
+        warm_up(kw, 7)
         k0 = bank(4, F32)
-        t_one(T["x00"], k0, 0)
+        t_pair(T["wg0"], k0)
         k1 = bank(5, F32)
-        t_one(T["wg0"], k1, 0)
-        t_one(T["wg0"], k1, 1)
+        t_pair(T["x00"], k1)
+        warm_up(kw, 1)
+        c_pair(k0, "wg0", "v")
         k2 = bank(6, F32)
-        t_one(T["wg1"], k2, 0)
-        t_one(T["wg1"], k2, 1)
-        t_one(T["wg1"], k2, 2)
-        t_one(T["x00"], k0, 1)
-        t_one(T["wg1"], k2, 3)
-        t_one(T["x00"], k0, 2)
-        t_one(T["wg0"], k1, 2)
-        t_one(T["wg0"], k1, 3)
+        t_pair(T["wg1"], k2)
+        warm_up(kw, 1)
+        c_pair(k1, "x00", "s")
         k3 = bank(7, F32)
-        t_one(T["x01"], k3, 0)
+        t_pair(T["x01"], k3)
         c_pair(k2, "wg1", "v")
-        t_one(T["x00"], k0, 3)
-        t_one(T["x01"], k3, 1)
-        t_one(T["x01"], k3, 2)
-        t_one(T["x01"], k3, 3)
-        c_pair(k0, "x00", "s")
-        c_pair(k1, "wg0", "v")
-        c_pair(k3, "x01", "s")
-        deg_f(0, deg[0][:, 0:1])
         k4 = bank(0, F32)
-        h_one(k4, 0, 1, 0)
-        h_one(k4, 0, 1, 1)
-        h_one(k4, 0, 1, 2)
+        h_grp(k4, 0, 0, 0)
+        h_grp(k4, 0, 1, 0)
+        c_pair(k3, "x01", "s")
         k5 = bank(1, F32)
-        h_one(k5, 0, 0, 0)
-        deg_f(3, deg[0][:, 3:4])
+        h_grp(k5, 0, 0, 1)
+        h_grp(k5, 0, 1, 1)
+        deg_f(0, deg[0][:, 0:1])
         k6 = bank(2, F32)
-        h_one(k6, 0, 2, 0)
+        h_grp(k6, 0, 0, 2)
+        h_grp(k6, 0, 1, 2)
         deg_f(1, deg[0][:, 1:2])
-        k7 = bank(6, F32)
-        t_one(T["x10"], k7, 0)
-        k8 = bank(3, F32)
-        h_one(k8, 0, 3, 0)
+        k7 = bank(3, F32)
+        h_grp(k7, 0, 0, 3)
+        h_grp(k7, 0, 1, 3)
         deg_f(2, deg[0][:, 2:3])
-        h_one(k6, 0, 2, 1)
-        t_one(T["x10"], k7, 1)
-        h_one(k6, 0, 2, 2)
+        h_grp(k4, 0, 2, 0)
+        h_grp(k4, 0, 3, 0)
+        deg_f(3, deg[0][:, 3:4])
         nc.vector.tensor_scalar_add(rec[0][:], deg[0][:], 1e-8)
         nc.vector.reciprocal(rec[0][:], rec[0][:])
-        deg_f(4, deg[1][:, 0:1])
-        t_one(T["x10"], k7, 2)
-        t_one(T["x10"], k7, 3)
-        h_one(k4, 0, 1, 3)
+        h_grp(k5, 0, 2, 1)
+        h_grp(k5, 0, 3, 1)
         d_sq(0)
-        h_one(k8, 0, 3, 1)
-        c_pair(k7, "x10", "s")
+        deg_f(4, deg[1][:, 0:1])
+        h_out(k4, 0, 0, "s")
+        k8 = bank(4, F32)
+        t_pair(T["x10"], k8)
         deg_f(5, deg[1][:, 1:2])
-        dj[0] = bank(4, F32)
-        t_dj_one(0, 0)
-        t_dj_one(0, 1)
-        h_one(k6, 0, 2, 3)
-        h_one(k5, 0, 0, 1)
-        deg_f(6, deg[1][:, 2:3])
-        t_dj_one(0, 2)
-        t_dj_one(0, 3)
-        h_one(k8, 0, 3, 2)
+        dj[0] = bank(5, F32)
+        t_dj(0)
+        h_out(k5, 0, 1, "s")
+        h_grp(k6, 0, 2, 2)
+        h_grp(k6, 0, 3, 2)
+        c_pair(k8, "x10", "s")
+        sc(0, 0)
+        h_grp(k7, 0, 2, 3)
+        h_grp(k7, 0, 3, 3)
         h_out(k6, 0, 2, "s")
-        h_one(k8, 0, 3, 3)
+        deg_f(6, deg[1][:, 2:3])
+        k9 = bank(0, F32)
+        h_grp(k9, 1, 0, 0)
+        h_grp(k9, 1, 1, 0)
+        sc(1, 0)
+        k10 = bank(1, F32)
+        h_grp(k10, 1, 0, 1)
+        h_grp(k10, 1, 1, 1)
         deg_f(7, deg[1][:, 3:4])
-        h_one(k5, 0, 0, 2)
-        h_out(k4, 0, 1, "s")
         nc.vector.tensor_scalar_add(rec[1][:], deg[1][:], 1e-8)
         nc.vector.reciprocal(rec[1][:], rec[1][:])
-        sc(1, 0)
-        k9 = bank(5, F32)
-        t_one(T["x11"], k9, 0)
-        h_one(k5, 0, 0, 3)
-        d_sq(1)
-        t_one(T["x11"], k9, 1)
-        t_one(T["x11"], k9, 2)
-        k10 = bank(2, F32)
-        h_one(k10, 1, 0, 0)
-        t_one(T["x11"], k9, 3)
         sc(2, 0)
-        h_one(k10, 1, 0, 1)
-        h_out(k5, 0, 0, "s")
-        dj[1] = bank(7, F32)
-        t_dj_one(1, 0)
-        h_one(k10, 1, 0, 2)
-        c_pair(k9, "x11", "s")
-        t_dj_one(1, 1)
-        k11 = bank(6, F32)
-        t_one(T["ws1"], k11, 0)
+        d_sq(1)
+        h_out(k7, 0, 3, "s")
+        dj[1] = bank(6, F32)
+        t_dj(1)
         sc(3, 0)
-        k12 = bank(0, F32)
-        h_one(k12, 1, 1, 0)
-        t_one(T["ws1"], k11, 1)
-        h_one(k12, 1, 1, 1)
-        h_out(k8, 0, 3, "s")
-        t_one(T["ws1"], k11, 2)
-        t_one(T["ws1"], k11, 3)
-        h_one(k12, 1, 1, 2)
-        sc(5, 0)
-        k13 = bank(5, F32)
-        t_one(T["ws0"], k13, 0)
-        t_one(T["ws0"], k13, 1)
-        h_one(k10, 1, 0, 3)
-        c_pair(k11, "ws1", "s")
-        t_one(T["ws0"], k13, 2)
-        t_one(T["ws0"], k13, 3)
-        k14 = bank(1, F32)
-        h_one(k14, 1, 2, 0)
-        rg(0, 1, "g")
-        sc(4, 0)
-        h_one(k14, 1, 2, 1)
-        h_out(k10, 1, 0, "s")
-        t_dj_one(1, 2)
-        t_dj_one(1, 3)
-        h_one(k14, 1, 2, 2)
-        sc(0, 0)
-        h_one(k14, 1, 2, 3)
-        c_pair(k13, "ws0", "s")
-        h_one(k12, 1, 1, 3)
+        k11 = bank(7, F32)
+        t_pair(T["x11"], k11)
+        k12 = bank(2, F32)
+        h_grp(k12, 1, 0, 2)
+        h_grp(k12, 1, 1, 2)
         sc(0, 1)
-        k15 = bank(6, BF16)
-        at_one(k15, 0, 0)
-        k16 = bank(4, BF16)
-        at_one(k16, 1, 0)
-        at_one(k16, 1, 1)
-        at_one(k15, 0, 1)
-        rg(0, 0, "g")
-        at_one(k16, 1, 2)
-        h_out(k14, 1, 2, "s")
-        at_one(k15, 0, 2)
-        at_one(k15, 0, 3)
-        k17 = bank(3, F32)
-        h_one(k17, 1, 3, 0)
+        c_pair(k11, "x11", "s")
+        k13 = bank(3, F32)
+        h_grp(k13, 1, 0, 3)
+        h_grp(k13, 1, 1, 3)
         sc(1, 1)
-        at_one(k15, 0, 4)
-        k18 = bank(5, F32)
-        t_one(T["x45"], k18, 0)
-        at_one(k15, 0, 5)
-        at_one(k15, 0, 6)
-        h_out(k12, 1, 1, "s")
-        at_one(k15, 0, 7)
-        h_one(k17, 1, 3, 1)
-        sc(3, 1)
-        at_one(k16, 1, 3)
-        t_one(T["x45"], k18, 1)
-        h_one(k17, 1, 3, 2)
-        a_out(k15, 0, "s")
-        k19 = bank(2, F32)
-        sk_one(k19, 0, 0)
-        sc(5, 1)
-        t_one(T["x45"], k18, 2)
-        t_one(T["x45"], k18, 3)
-        k20 = bank(1, F32)
-        sk_one(k20, 2, 0)
-        h_one(k17, 1, 3, 3)
-        sk_one(k20, 2, 1)
-        sc(4, 1)
-        c_pair(k18, "x45", "s")
-        k21 = bank(6, BF16)
-        at_one(k21, 3, 0)
-        sk_one(k20, 2, 2)
-        k22 = bank(0, F32)
-        sk_one(k22, 1, 0)
-        sc(2, 1)
-        h_out(k17, 1, 3, "s")
-        k23 = bank(5, BF16)
-        at_one(k23, 4, 0)
-        at_one(k21, 3, 1)
-        at_one(k21, 3, 2)
-        at_one(k21, 3, 3)
-        at_one(k16, 1, 4)
-        sk_one(k22, 1, 1)
+        k14 = bank(4, F32)
+        t_pair(T["ws0"], k14)
         q_h(0)
-        rg(1, 1, "s")
-        at_one(k16, 1, 5)
-        at_one(k16, 1, 6)
-        at_one(k23, 4, 1)
-        k24 = bank(7, BF16)
-        at_one(k24, 2, 0)
-        at_one(k23, 4, 2)
-        at_one(k16, 1, 7)
-        sk_one(k19, 0, 1)
+        h_grp(k9, 1, 2, 0)
+        h_grp(k9, 1, 3, 0)
+        c_pair(k14, "ws0", "s")
+        sc(2, 1)
+        k15 = bank(7, F32)
+        t_pair(T["ws1"], k15)
+        h_out(k9, 1, 0, "s")
+        h_grp(k10, 1, 2, 1)
+        h_grp(k10, 1, 3, 1)
+        sc(3, 1)
+        c_pair(k15, "ws1", "s")
+        h_grp(k12, 1, 2, 2)
+        h_grp(k12, 1, 3, 2)
+        sc(4, 0)
+        h_out(k10, 1, 1, "s")
+        h_grp(k13, 1, 2, 3)
+        h_grp(k13, 1, 3, 3)
+        sc(4, 1)
+        h_out(k12, 1, 2, "s")
+        k16 = bank(4, F32)
+        t_pair(T["x45"], k16)
+        sc(5, 0)
+        k17 = bank(7, BF16)
+        at_one(k17, 0, 0)
+        at_one(k17, 0, 1)
+        h_out(k13, 1, 3, "s")
+        at_one(k17, 0, 2)
+        at_one(k17, 0, 3)
+        at_one(k17, 0, 4)
+        at_one(k17, 0, 5)
+        at_one(k17, 0, 6)
+        sc(5, 1)
+        at_one(k17, 0, 7)
+        k18 = bank(0, F32)
+        sk_one(k18, 0, 0)
+        c_pair(k16, "x45", "s")
+        k19 = bank(5, BF16)
+        at_one(k19, 1, 0)
+        at_one(k19, 1, 1)
+        at_one(k19, 1, 2)
+        sk_one(k18, 0, 1)
+        at_one(k19, 1, 3)
+        at_one(k19, 1, 4)
+        at_one(k19, 1, 5)
+        sk_one(k18, 0, 2)
+        a_out(k17, 0, "s")
+        at_one(k19, 1, 6)
+        at_one(k19, 1, 7)
+        k20 = bank(6, BF16)
+        at_one(k20, 2, 0)
+        sk_one(k18, 0, 3)
+        at_one(k20, 2, 1)
+        at_one(k20, 2, 2)
+        at_one(k20, 2, 3)
+        k21 = bank(1, F32)
+        sk_one(k21, 1, 0)
+        at_one(k20, 2, 4)
+        at_one(k20, 2, 5)
+        at_one(k20, 2, 6)
+        sk_one(k21, 1, 1)
+        a_out(k19, 1, "s")
+        at_one(k20, 2, 7)
+        k22 = bank(4, BF16)
+        at_one(k22, 3, 0)
+        at_one(k22, 3, 1)
         q_a(0)
-        at_one(k24, 2, 1)
-        at_one(k24, 2, 2)
-        at_one(k21, 3, 4)
-        at_one(k24, 2, 3)
-        at_one(k23, 4, 3)
-        at_one(k23, 4, 4)
-        sk_one(k19, 0, 2)
-        rg(1, 0, "v")
-        at_one(k21, 3, 5)
-        sk_one(k19, 0, 3)
-        a_out(k16, 1, "s")
-        at_one(k24, 2, 4)
-        sk_one(k22, 1, 2)
+        sk_one(k21, 1, 2)
+        at_one(k22, 3, 2)
+        at_one(k22, 3, 3)
         q_h(1)
-        at_one(k24, 2, 5)
-        at_one(k21, 3, 6)
-        sk_one(k20, 2, 3)
-        at_one(k23, 4, 5)
-        sk_one(k22, 1, 3)
-        s_out(k19, 0)
+        at_one(k22, 3, 4)
+        sk_one(k21, 1, 3)
+        at_one(k22, 3, 5)
+        at_one(k22, 3, 6)
+        at_one(k22, 3, 7)
+        s_out(k18, 0)
         q_a(1)
-        k25 = bank(3, F32)
-        mx(k25, 0)
-        s_out(k22, 1)
-        k26 = bank(2, F32)
-        sk_one(k26, 3, 0)
-        at_one(k24, 2, 6)
-        at_one(k21, 3, 7)
-        at_one(k24, 2, 7)
-        e1(k25, 0)
-        k27 = bank(4, BF16)
-        at_one(k27, 5, 0)
-        s_out(k20, 2)
-        sk_one(k26, 3, 1)
-        at_one(k27, 5, 1)
-        at_one(k27, 5, 2)
-        sk_one(k26, 3, 2)
-        a_out(k21, 3, "s")
-        a_out(k24, 2, "v")
-        at_one(k27, 5, 3)
-        at_one(k27, 5, 4)
-        k28 = bank(0, F32)
-        mx(k28, 1)
-        e2g(0)
-        sk_one(k26, 3, 3)
-        at_one(k27, 5, 5)
-        at_one(k23, 4, 6)
-        k29 = bank(1, F32)
-        sk_one(k29, 5, 0)
+        k23 = bank(2, F32)
+        mx(k23, 0)
+        a_out(k20, 2, "s")
+        k24 = bank(3, F32)
+        sk_one(k24, 2, 0)
+        k25 = bank(7, BF16)
+        at_one(k25, 4, 0)
+        at_one(k25, 4, 1)
+        at_one(k25, 4, 2)
+        sk_one(k24, 2, 1)
+        at_one(k25, 4, 3)
+        at_one(k25, 4, 4)
+        at_one(k25, 4, 5)
+        sk_one(k24, 2, 2)
+        a_out(k22, 3, "s")
         q_a(2)
-        at_one(k23, 4, 7)
-        s_out(k26, 3)
-        at_one(k27, 5, 6)
-        at_one(k27, 5, 7)
-        k30 = bank(3, F32)
-        sk_one(k30, 4, 0)
-        e1(k28, 1)
-        a_out(k23, 4, "s")
+        at_one(k25, 4, 6)
+        at_one(k25, 4, 7)
+        k26 = bank(5, BF16)
+        at_one(k26, 5, 0)
+        sk_one(k24, 2, 3)
+        e1(k23, 0)
+        at_one(k26, 5, 1)
+        at_one(k26, 5, 2)
+        at_one(k26, 5, 3)
+        k27 = bank(0, F32)
+        mx(k27, 1)
+        e2(0)
+        s_out(k21, 1)
+        k28 = bank(2, F32)
+        sk_one(k28, 3, 0)
+        at_one(k26, 5, 4)
+        at_one(k26, 5, 5)
+        at_one(k26, 5, 6)
+        sk_one(k28, 3, 1)
         q_a(3)
-        k31 = bank(2, F32)
-        mx(k31, 2)
-        e2g(1)
+        a_out(k25, 4, "s")
         st(0)
-        sk_one(k29, 5, 1)
-        k32 = bank(0, F32)
-        mx(k32, 3)
-        e1(k31, 2)
-        a_out(k27, 5, "s")
-        sk_one(k30, 4, 1)
+        at_one(k26, 5, 7)
+        sk_one(k28, 3, 2)
+        e1(k27, 1)
+        sk_one(k28, 3, 3)
+        k29 = bank(1, F32)
+        mx(k29, 2)
+        e2(1)
+        s_out(k24, 2)
+        k30 = bank(0, F32)
+        mx(k30, 3)
         q_a(4)
-        sk_one(k30, 4, 2)
-        e1(k32, 3)
-        sk_one(k30, 4, 3)
-        e2g(2)
-        sk_one(k29, 5, 2)
         st(1)
+        a_out(k26, 5, "s")
+        e1(k29, 2)
+        k31 = bank(3, F32)
+        sk_one(k31, 4, 0)
+        sk_one(k31, 4, 1)
+        e2(2)
+        sk_one(k31, 4, 2)
+        sk_one(k31, 4, 3)
+        s_out(k28, 3)
+        k32 = bank(1, F32)
+        mx(k32, 4)
         q_a(5)
-        k33 = bank(2, F32)
-        mx(k33, 4)
-        s_out(k30, 4)
-        e2(3)
-        sk_one(k29, 5, 3)
-        k34 = bank(0, F32)
-        mx(k34, 5)
-        e1(k33, 4)
-        s_out(k29, 5)
-        e2(4)
         st(2)
+        s_out(k31, 4)
+        e1(k30, 3)
+        k33 = bank(2, F32)
+        sk_one(k33, 5, 0)
+        sk_one(k33, 5, 1)
+        e2(3)
+        sk_one(k33, 5, 2)
+        sk_one(k33, 5, 3)
+        k34 = bank(3, F32)
+        mx(k34, 5)
+        e1(k32, 4)
         st(3)
+        s_out(k33, 5)
+        e2(4)
         e1(k34, 5)
         st(4)
         e2(5)

@@ -39,13 +39,6 @@ def tile_structureawaregcn_kernel(tc, adjacency_matrix, node_features, W_gcn, W_
         nc.vector.memset(warm[:], 1.0)
         nc.scalar.sqrt(warm[:], warm[:])
 
-        zeros_f = keep.tile([P, P], F32, name="zeros_f")
-        nc.vector.memset(zeros_f[:], 0.0)
-
-        def warm_up(bk, n):
-            for r in range(n):
-                nc.tensor.matmul(bk[:, 0:P], lhsT=zeros_f[:], rhs=zeros_f[:], start=True, stop=True)
-
         x_lo = node_features[0:512, :].rearrange("(p t) c -> p t c", t=4)
         x_hi = node_features[512:1024, :].rearrange("(p t) c -> p t c", t=4)
         a_lo = adjacency_matrix[0:512, :].rearrange("(p t) j -> p t j", t=4)
@@ -261,17 +254,13 @@ def tile_structureawaregcn_kernel(tc, adjacency_matrix, node_features, W_gcn, W_
         ld("ws0")
         ld("ws1")
         ld("x45")
-        kw = bank(7, F32)
-        warm_up(kw, 7)
         k0 = bank(4, F32)
         t_pair(T["wg0"], k0)
         k1 = bank(5, F32)
         t_pair(T["x00"], k1)
-        warm_up(kw, 1)
         c_pair(k0, "wg0", "v")
         k2 = bank(6, F32)
         t_pair(T["wg1"], k2)
-        warm_up(kw, 1)
         c_pair(k1, "x00", "s")
         k3 = bank(7, F32)
         t_pair(T["x01"], k3)
@@ -310,65 +299,64 @@ def tile_structureawaregcn_kernel(tc, adjacency_matrix, node_features, W_gcn, W_
         h_out(k5, 0, 1, "s")
         h_grp(k6, 0, 2, 2)
         h_grp(k6, 0, 3, 2)
+        deg_f(6, deg[1][:, 2:3])
         c_pair(k8, "x10", "s")
-        sc(0, 0)
         h_grp(k7, 0, 2, 3)
         h_grp(k7, 0, 3, 3)
+        deg_f(7, deg[1][:, 3:4])
         h_out(k6, 0, 2, "s")
-        deg_f(6, deg[1][:, 2:3])
         k9 = bank(0, F32)
         h_grp(k9, 1, 0, 0)
         h_grp(k9, 1, 1, 0)
-        sc(1, 0)
+        nc.vector.tensor_scalar_add(rec[1][:], deg[1][:], 1e-8)
+        nc.vector.reciprocal(rec[1][:], rec[1][:])
+        sc(0, 0)
+        d_sq(1)
+        h_out(k7, 0, 3, "s")
         k10 = bank(1, F32)
         h_grp(k10, 1, 0, 1)
         h_grp(k10, 1, 1, 1)
-        deg_f(7, deg[1][:, 3:4])
-        nc.vector.tensor_scalar_add(rec[1][:], deg[1][:], 1e-8)
-        nc.vector.reciprocal(rec[1][:], rec[1][:])
-        sc(2, 0)
-        d_sq(1)
-        h_out(k7, 0, 3, "s")
-        dj[1] = bank(6, F32)
-        t_dj(1)
-        sc(3, 0)
-        k11 = bank(7, F32)
+        sc(1, 0)
+        k11 = bank(6, F32)
         t_pair(T["x11"], k11)
+        sc(2, 0)
+        dj[1] = bank(7, F32)
+        t_dj(1)
+        c_pair(k11, "x11", "s")
         k12 = bank(2, F32)
         h_grp(k12, 1, 0, 2)
         h_grp(k12, 1, 1, 2)
-        sc(0, 1)
-        c_pair(k11, "x11", "s")
+        sc(3, 0)
         k13 = bank(3, F32)
         h_grp(k13, 1, 0, 3)
         h_grp(k13, 1, 1, 3)
-        sc(1, 1)
+        sc(0, 1)
         k14 = bank(4, F32)
         t_pair(T["ws0"], k14)
-        q_h(0)
+        sc(1, 1)
         h_grp(k9, 1, 2, 0)
         h_grp(k9, 1, 3, 0)
         c_pair(k14, "ws0", "s")
-        sc(2, 1)
-        k15 = bank(7, F32)
+        q_h(0)
+        k15 = bank(6, F32)
         t_pair(T["ws1"], k15)
         h_out(k9, 1, 0, "s")
         h_grp(k10, 1, 2, 1)
         h_grp(k10, 1, 3, 1)
-        sc(3, 1)
+        sc(2, 1)
         c_pair(k15, "ws1", "s")
         h_grp(k12, 1, 2, 2)
         h_grp(k12, 1, 3, 2)
-        sc(4, 0)
+        sc(3, 1)
         h_out(k10, 1, 1, "s")
         h_grp(k13, 1, 2, 3)
         h_grp(k13, 1, 3, 3)
-        sc(4, 1)
+        sc(4, 0)
         h_out(k12, 1, 2, "s")
         k16 = bank(4, F32)
         t_pair(T["x45"], k16)
-        sc(5, 0)
-        k17 = bank(7, BF16)
+        sc(4, 1)
+        k17 = bank(6, BF16)
         at_one(k17, 0, 0)
         at_one(k17, 0, 1)
         h_out(k13, 1, 3, "s")
@@ -377,11 +365,13 @@ def tile_structureawaregcn_kernel(tc, adjacency_matrix, node_features, W_gcn, W_
         at_one(k17, 0, 4)
         at_one(k17, 0, 5)
         at_one(k17, 0, 6)
-        sc(5, 1)
         at_one(k17, 0, 7)
+        sc(5, 0)
         k18 = bank(0, F32)
         sk_one(k18, 0, 0)
         c_pair(k16, "x45", "s")
+        sc(5, 1)
+        a_out(k17, 0, "s")
         k19 = bank(5, BF16)
         at_one(k19, 1, 0)
         at_one(k19, 1, 1)
@@ -391,10 +381,10 @@ def tile_structureawaregcn_kernel(tc, adjacency_matrix, node_features, W_gcn, W_
         at_one(k19, 1, 4)
         at_one(k19, 1, 5)
         sk_one(k18, 0, 2)
-        a_out(k17, 0, "s")
+        q_h(1)
         at_one(k19, 1, 6)
         at_one(k19, 1, 7)
-        k20 = bank(6, BF16)
+        k20 = bank(4, BF16)
         at_one(k20, 2, 0)
         sk_one(k18, 0, 3)
         at_one(k20, 2, 1)
@@ -402,33 +392,32 @@ def tile_structureawaregcn_kernel(tc, adjacency_matrix, node_features, W_gcn, W_
         at_one(k20, 2, 3)
         k21 = bank(1, F32)
         sk_one(k21, 1, 0)
+        a_out(k19, 1, "s")
+        q_a(0)
         at_one(k20, 2, 4)
         at_one(k20, 2, 5)
         at_one(k20, 2, 6)
         sk_one(k21, 1, 1)
-        a_out(k19, 1, "s")
         at_one(k20, 2, 7)
-        k22 = bank(4, BF16)
+        k22 = bank(7, BF16)
         at_one(k22, 3, 0)
         at_one(k22, 3, 1)
-        q_a(0)
         sk_one(k21, 1, 2)
         at_one(k22, 3, 2)
         at_one(k22, 3, 3)
-        q_h(1)
         at_one(k22, 3, 4)
         sk_one(k21, 1, 3)
+        s_out(k18, 0)
         at_one(k22, 3, 5)
         at_one(k22, 3, 6)
         at_one(k22, 3, 7)
-        s_out(k18, 0)
-        q_a(1)
         k23 = bank(2, F32)
         mx(k23, 0)
+        q_a(1)
         a_out(k20, 2, "s")
         k24 = bank(3, F32)
         sk_one(k24, 2, 0)
-        k25 = bank(7, BF16)
+        k25 = bank(6, BF16)
         at_one(k25, 4, 0)
         at_one(k25, 4, 1)
         at_one(k25, 4, 2)
@@ -438,18 +427,18 @@ def tile_structureawaregcn_kernel(tc, adjacency_matrix, node_features, W_gcn, W_
         at_one(k25, 4, 5)
         sk_one(k24, 2, 2)
         a_out(k22, 3, "s")
-        q_a(2)
         at_one(k25, 4, 6)
         at_one(k25, 4, 7)
         k26 = bank(5, BF16)
         at_one(k26, 5, 0)
         sk_one(k24, 2, 3)
-        e1(k23, 0)
+        q_a(2)
         at_one(k26, 5, 1)
         at_one(k26, 5, 2)
         at_one(k26, 5, 3)
         k27 = bank(0, F32)
         mx(k27, 1)
+        e1(k23, 0)
         e2(0)
         s_out(k21, 1)
         k28 = bank(2, F32)
@@ -460,8 +449,8 @@ def tile_structureawaregcn_kernel(tc, adjacency_matrix, node_features, W_gcn, W_
         sk_one(k28, 3, 1)
         q_a(3)
         a_out(k25, 4, "s")
-        st(0)
         at_one(k26, 5, 7)
+        st(0)
         sk_one(k28, 3, 2)
         e1(k27, 1)
         sk_one(k28, 3, 3)
@@ -474,12 +463,12 @@ def tile_structureawaregcn_kernel(tc, adjacency_matrix, node_features, W_gcn, W_
         q_a(4)
         st(1)
         a_out(k26, 5, "s")
-        e1(k29, 2)
         k31 = bank(3, F32)
         sk_one(k31, 4, 0)
+        e1(k29, 2)
         sk_one(k31, 4, 1)
-        e2(2)
         sk_one(k31, 4, 2)
+        e2(2)
         sk_one(k31, 4, 3)
         s_out(k28, 3)
         k32 = bank(1, F32)
@@ -487,12 +476,12 @@ def tile_structureawaregcn_kernel(tc, adjacency_matrix, node_features, W_gcn, W_
         q_a(5)
         st(2)
         s_out(k31, 4)
-        e1(k30, 3)
         k33 = bank(2, F32)
         sk_one(k33, 5, 0)
+        e1(k30, 3)
         sk_one(k33, 5, 1)
-        e2(3)
         sk_one(k33, 5, 2)
+        e2(3)
         sk_one(k33, 5, 3)
         k34 = bank(3, F32)
         mx(k34, 5)

@@ -33,27 +33,24 @@ def tile_structureawaregcn_kernel(tc, adjacency_matrix, node_features, W_gcn, W_
 
         ident_f = keep.tile([P, P], F32, name="ident_f")
         make_identity(nc, ident_f[:])
-        ident_b = keep.tile([P, P], BF16, name="ident_b")
-        make_identity(nc, ident_b[:])
         warm = keep.tile([P, 1], F32, name="warm")
         nc.vector.memset(warm[:], 1.0)
         nc.scalar.sqrt(warm[:], warm[:])
 
-        x_lo = node_features[0:512, :].rearrange("(p t) c -> p t c", t=4)
-        x_hi = node_features[512:1024, :].rearrange("(p t) c -> p t c", t=4)
-        a_lo = adjacency_matrix[0:512, :].rearrange("(p t) j -> p t j", t=4)
+        x_lo = node_features[0:512, :].rearrange("(u p e) c -> p u e c", u=2, e=2)
+        x_hi = node_features[512:1024, :].rearrange("(h u p) c -> p u h c", h=2, u=2)
+        a_lo = adjacency_matrix[0:512, :].rearrange("(u p e) j -> p u e j", u=2, e=2)
         SRC = {
             "wg0": W_gcn[0:256, :].rearrange("(m p) c -> p m c", p=P),
             "wg1": W_gcn[256:512, :].rearrange("(m p) c -> p m c", p=P),
             "ws0": W_skip[0:256, :].rearrange("(m p) c -> p m c", p=P),
             "ws1": W_skip[256:512, :].rearrange("(m p) c -> p m c", p=P),
-            "x00": x_lo[:, 0:2, :],
-            "x01": x_lo[:, 2:4, :],
-            "x10": x_hi[:, 0:2, :],
-            "x11": x_hi[:, 2:4, :],
-            "x45": node_features[512:768, :].rearrange("(m p) c -> p m c", p=P),
-            "a03_0": a_lo[:, 0:2, :],
-            "a03_1": a_lo[:, 2:4, :],
+            "x00": x_lo[:, 0, :, :],
+            "x01": x_lo[:, 1, :, :],
+            "x10": x_hi[:, 0, :, :],
+            "x11": x_hi[:, 1, :, :],
+            "a03_0": a_lo[:, 0, :, :],
+            "a03_1": a_lo[:, 1, :, :],
         }
         T = {}
         a_rows = {}
@@ -105,10 +102,11 @@ def tile_structureawaregcn_kernel(tc, adjacency_matrix, node_features, W_gcn, W_
         def h_grp(bk, g, t, oc):
             xt = PAIRS["x%d%d" % (g, t // 2)]
             wt = PAIRS["wg%d" % (oc // 2)]
+            cols = slice((t % 2) * P, (t % 2 + 1) * P) if g == 0 else slice(t % 2, 2 * P, 2)
             for ci, (u, e) in enumerate(CHUNKS):
                 nc.tensor.matmul(
                     bk[:, t * P : (t + 1) * P],
-                    lhsT=xt[:, u, (t % 2) * P : (t % 2 + 1) * P, e],
+                    lhsT=xt[:, u, cols, e],
                     rhs=wt[:, u, (oc % 2) * P : (oc % 2 + 1) * P, e],
                     start=(ci == 0),
                     stop=(ci == 3),
@@ -164,16 +162,26 @@ def tile_structureawaregcn_kernel(tc, adjacency_matrix, node_features, W_gcn, W_
         ahat = [keep.tile([P, N_NODES], BF16, name="ahat%d" % m) for m in range(6)]
 
         def sc(m, g):
-            in1 = dj[g][:].rearrange("i (t p) -> i t p", t=4) if g == 0 else dj[g][:].rearrange("i (p t) -> i t p", t=4)
             c = m % 4
-            nc.vector.scalar_tensor_tensor(
-                out=ahat[m][:, g * 512 : (g + 1) * 512].rearrange("i (t p) -> i t p", t=4),
-                in0=a_rows[m][:, g * 512 : (g + 1) * 512].rearrange("i (p t) -> i t p", t=4),
-                scalar=dcol[m // 4][:, c : c + 1],
-                in1=in1,
-                op0=ALU.mult,
-                op1=ALU.mult,
-            )
+            for u in range(2):
+                dst = ahat[m][:, g * 512 + u * 256 : g * 512 + (u + 1) * 256]
+                src = a_rows[m][:, g * 512 : (g + 1) * 512]
+                if g == 0:
+                    dst_v = dst.rearrange("i (p e) -> i p e", e=2)
+                    src_v = src[:, u * 256 : (u + 1) * 256].rearrange("i (p e) -> i p e", e=2)
+                    in1 = dj[0][:, u * 256 : (u + 1) * 256].rearrange("i (e p) -> i p e", e=2)
+                else:
+                    dst_v = dst.rearrange("i (h x) -> i h x", h=2)
+                    src_v = src.rearrange("i (h u x) -> i u h x", h=2, u=2)[:, u, :, :]
+                    in1 = dj[1][:].rearrange("i (h u x) -> i u h x", h=2, u=2)[:, u, :, :]
+                nc.vector.scalar_tensor_tensor(
+                    out=dst_v,
+                    in0=src_v,
+                    scalar=dcol[m // 4][:, c : c + 1],
+                    in1=in1,
+                    op0=ALU.mult,
+                    op1=ALU.mult,
+                )
 
         agrp = [keep.tile([P, N_NODES], BF16, name="agrp%d" % m, align_bytes=64) for m in range(6)]
         acodes = [keep.tile([P, 256], U32, name="acodes%d" % m, align_bytes=64) for m in range(6)]
@@ -182,12 +190,13 @@ def tile_structureawaregcn_kernel(tc, adjacency_matrix, node_features, W_gcn, W_
         pre = [keep.tile([P, D], F32, name="pre%d" % m) for m in range(6)]
         fin = [keep.tile([P, D], F32, name="fin%d" % m) for m in range(6)]
 
-        def at_one(bk, m, b):
-            nc.tensor.transpose(bk[:, b * P : (b + 1) * P], ahat[m][:, b * P : (b + 1) * P], ident_b[:])
+        def at_word(bk, m, b):
+            words = ahat[m][:].bitcast(F32)
+            nc.tensor.transpose(bk[:, b * P : (b + 1) * P], words[:, b * P : (b + 1) * P], ident_f[:])
 
         def a_out(bk, m, eng):
-            dst_v = agrp[m][:].rearrange("p (g i t) -> p g i t", g=2, t=4)
-            src_v = bk[:].rearrange("p (g t i) -> p g i t", g=2, t=4)
+            dst_v = agrp[m][:].bitcast(F32).rearrange("p (g i u) -> p g i u", g=2, u=2)
+            src_v = bk[:].rearrange("p (g u i) -> p g i u", g=2, u=2)
             if eng == "v":
                 nc.vector.tensor_copy(out=dst_v, in_=src_v)
             else:
@@ -197,8 +206,8 @@ def tile_structureawaregcn_kernel(tc, adjacency_matrix, node_features, W_gcn, W_
             nc.vector.quantize_mx(out=acodes[m][:].bitcast(FP8X4), scales=ascales[m][:], in_=agrp[m][:])
 
         def sk_one(bk, m, ci):
-            xt = PAIRS["x0%d" % (m // 2)] if m < 4 else PAIRS["x45"]
-            col = (m % 2) * P
+            xt = PAIRS["x0%d" % (m // 2)] if m < 4 else PAIRS["x1%d" % (m - 4)]
+            col = (m % 2) * P if m < 4 else 0
             u, e = CHUNKS[ci]
             nc.tensor.matmul(bk[:], lhsT=xt[:, u, col : col + P, e], rhs=wsT[:, u, :, e], start=(ci == 0), stop=(ci == 3))
 
@@ -217,24 +226,24 @@ def tile_structureawaregcn_kernel(tc, adjacency_matrix, node_features, W_gcn, W_
                     stop=(g == 1),
                 )
 
-        out03 = out[0:512, :].rearrange("(p t) o -> p t o", t=4)
+        out03 = out[0:512, :].rearrange("(u p e) o -> p u e o", u=2, e=2)
 
         def e1(bk, m):
             nc.vector.scalar_tensor_tensor(out=pre[m][:], in0=bk[:], scalar=0.5, in1=skip_sb[m][:], op0=ALU.mult, op1=ALU.add)
 
         def e2(m):
-            res = T["x0%d" % (m // 2)][:, (m % 2) * D : (m % 2 + 1) * D] if m < 4 else T["x45"][:, (m - 4) * D : (m - 3) * D]
+            res = T["x0%d" % (m // 2)][:, (m % 2) * D : (m % 2 + 1) * D] if m < 4 else T["x1%d" % (m - 4)][:, 0:D]
             nc.vector.scalar_tensor_tensor(out=fin[m][:], in0=pre[m][:], scalar=0.0, in1=res, op0=ALU.max, op1=ALU.add)
 
         def st(m):
-            dst = out03[:, m, :] if m < 4 else out[P * m : P * (m + 1), :]
+            dst = out03[:, m // 2, m % 2, :] if m < 4 else out[P * m : P * (m + 1), :]
             nc.sync.dma_start(out=dst, in_=fin[m][:])
 
         wsT_w = keep.tile([P, 8 * P], F32, name="wsT")
         wsT = pairs(wsT_w)
         WORDS = {}
         PAIRS = {}
-        for key in ["wg0", "wg1", "x00", "x01", "x10", "x11", "x45"]:
+        for key in ["wg0", "wg1", "x00", "x01", "x10", "x11"]:
             WORDS[key] = keep.tile([P, 4 * P], F32, name="w_" + key)
             PAIRS[key] = pairs(WORDS[key])
         deg = [keep.tile([P, 4], F32, name="deg%d" % h) for h in range(2)]
@@ -253,7 +262,6 @@ def tile_structureawaregcn_kernel(tc, adjacency_matrix, node_features, W_gcn, W_
         ld("x11")
         ld("ws0")
         ld("ws1")
-        ld("x45")
         k0 = bank(4, F32)
         t_pair(T["wg0"], k0)
         k1 = bank(5, F32)
@@ -353,89 +361,64 @@ def tile_structureawaregcn_kernel(tc, adjacency_matrix, node_features, W_gcn, W_
         h_grp(k13, 1, 3, 3)
         sc(4, 0)
         h_out(k12, 1, 2, "s")
-        k16 = bank(4, F32)
-        t_pair(T["x45"], k16)
         sc(4, 1)
-        k17 = bank(6, BF16)
-        at_one(k17, 0, 0)
-        at_one(k17, 0, 1)
+        k17 = bank(6, F32)
+        at_word(k17, 0, 0)
         h_out(k13, 1, 3, "s")
-        at_one(k17, 0, 2)
-        at_one(k17, 0, 3)
-        at_one(k17, 0, 4)
-        at_one(k17, 0, 5)
-        at_one(k17, 0, 6)
-        at_one(k17, 0, 7)
+        at_word(k17, 0, 1)
+        at_word(k17, 0, 2)
+        at_word(k17, 0, 3)
         sc(5, 0)
         k18 = bank(0, F32)
         sk_one(k18, 0, 0)
-        c_pair(k16, "x45", "s")
         sc(5, 1)
         a_out(k17, 0, "s")
-        k19 = bank(5, BF16)
-        at_one(k19, 1, 0)
-        at_one(k19, 1, 1)
-        at_one(k19, 1, 2)
+        k19 = bank(5, F32)
+        at_word(k19, 1, 0)
         sk_one(k18, 0, 1)
-        at_one(k19, 1, 3)
-        at_one(k19, 1, 4)
-        at_one(k19, 1, 5)
+        at_word(k19, 1, 1)
+        at_word(k19, 1, 2)
         sk_one(k18, 0, 2)
         q_h(1)
-        at_one(k19, 1, 6)
-        at_one(k19, 1, 7)
-        k20 = bank(4, BF16)
-        at_one(k20, 2, 0)
+        at_word(k19, 1, 3)
+        k20 = bank(4, F32)
         sk_one(k18, 0, 3)
-        at_one(k20, 2, 1)
-        at_one(k20, 2, 2)
-        at_one(k20, 2, 3)
+        at_word(k20, 2, 0)
+        at_word(k20, 2, 1)
         k21 = bank(1, F32)
         sk_one(k21, 1, 0)
         a_out(k19, 1, "s")
         q_a(0)
-        at_one(k20, 2, 4)
-        at_one(k20, 2, 5)
-        at_one(k20, 2, 6)
+        at_word(k20, 2, 2)
         sk_one(k21, 1, 1)
-        at_one(k20, 2, 7)
-        k22 = bank(7, BF16)
-        at_one(k22, 3, 0)
-        at_one(k22, 3, 1)
+        at_word(k20, 2, 3)
+        k22 = bank(7, F32)
+        at_word(k22, 3, 0)
         sk_one(k21, 1, 2)
-        at_one(k22, 3, 2)
-        at_one(k22, 3, 3)
-        at_one(k22, 3, 4)
+        at_word(k22, 3, 1)
         sk_one(k21, 1, 3)
         s_out(k18, 0)
-        at_one(k22, 3, 5)
-        at_one(k22, 3, 6)
-        at_one(k22, 3, 7)
+        at_word(k22, 3, 2)
+        at_word(k22, 3, 3)
         k23 = bank(2, F32)
         mx(k23, 0)
         q_a(1)
         a_out(k20, 2, "s")
         k24 = bank(3, F32)
         sk_one(k24, 2, 0)
-        k25 = bank(6, BF16)
-        at_one(k25, 4, 0)
-        at_one(k25, 4, 1)
-        at_one(k25, 4, 2)
+        k25 = bank(6, F32)
+        at_word(k25, 4, 0)
         sk_one(k24, 2, 1)
-        at_one(k25, 4, 3)
-        at_one(k25, 4, 4)
-        at_one(k25, 4, 5)
+        at_word(k25, 4, 1)
+        at_word(k25, 4, 2)
         sk_one(k24, 2, 2)
         a_out(k22, 3, "s")
-        at_one(k25, 4, 6)
-        at_one(k25, 4, 7)
-        k26 = bank(5, BF16)
-        at_one(k26, 5, 0)
+        at_word(k25, 4, 3)
+        k26 = bank(5, F32)
         sk_one(k24, 2, 3)
         q_a(2)
-        at_one(k26, 5, 1)
-        at_one(k26, 5, 2)
-        at_one(k26, 5, 3)
+        at_word(k26, 5, 0)
+        at_word(k26, 5, 1)
         k27 = bank(0, F32)
         mx(k27, 1)
         e1(k23, 0)
@@ -443,13 +426,11 @@ def tile_structureawaregcn_kernel(tc, adjacency_matrix, node_features, W_gcn, W_
         s_out(k21, 1)
         k28 = bank(2, F32)
         sk_one(k28, 3, 0)
-        at_one(k26, 5, 4)
-        at_one(k26, 5, 5)
-        at_one(k26, 5, 6)
+        at_word(k26, 5, 2)
         sk_one(k28, 3, 1)
         q_a(3)
         a_out(k25, 4, "s")
-        at_one(k26, 5, 7)
+        at_word(k26, 5, 3)
         st(0)
         sk_one(k28, 3, 2)
         e1(k27, 1)

@@ -28,449 +28,354 @@ def tile_structureawaregcn_kernel(tc, adjacency_matrix, node_features, W_gcn, W_
         psum = ctx.enter_context(tc.psum_pool(name="psum", bufs=1))
         ctx.enter_context(tc.manual_schedule())
 
-        def bank(i, dtype):
-            return psum.tile([P, 512 if dtype == F32 else 1024], dtype, name="bk%d" % i, tag="bk%d" % i)
+        def bank(i):
+            return psum.tile([P, 512], F32, name="bk%d" % i, tag="bk%d" % i)
 
-        ident_f = keep.tile([P, P], F32, name="ident_f")
-        make_identity(nc, ident_f[:])
         warm = keep.tile([P, 1], F32, name="warm")
         nc.vector.memset(warm[:], 1.0)
         nc.scalar.sqrt(warm[:], warm[:])
+        ident = keep.tile([P, P], F32, name="ident")
+        make_identity(nc, ident[:])
 
         x_lo = node_features[0:512, :].rearrange("(u p e) c -> p u e c", u=2, e=2)
         x_hi = node_features[512:1024, :].rearrange("(h u p) c -> p u h c", h=2, u=2)
         a_lo = adjacency_matrix[0:512, :].rearrange("(u p e) j -> p u e j", u=2, e=2)
-        SRC = {
-            "wg0": W_gcn[0:256, :].rearrange("(m p) c -> p m c", p=P),
-            "wg1": W_gcn[256:512, :].rearrange("(m p) c -> p m c", p=P),
-            "ws0": W_skip[0:256, :].rearrange("(m p) c -> p m c", p=P),
-            "ws1": W_skip[256:512, :].rearrange("(m p) c -> p m c", p=P),
-            "x00": x_lo[:, 0, :, :],
-            "x01": x_lo[:, 1, :, :],
-            "x10": x_hi[:, 0, :, :],
-            "x11": x_hi[:, 1, :, :],
-            "a03_0": a_lo[:, 0, :, :],
-            "a03_1": a_lo[:, 1, :, :],
-        }
-        T = {}
-        a_rows = {}
+        out_lo = out[0:512, :].rearrange("(u p e) o -> p u e o", u=2, e=2)
 
-        def ld(key):
-            if key in SRC:
-                src = SRC[key]
-                width = src.shape[1] * src.shape[2]
-                t = keep.tile([P, width], BF16, name="in_" + key)
-                nc.sync.dma_start(out=t[:].rearrange("p (a b) -> p a b", a=2), in_=src)
-                if key == "a03_0" or key == "a03_1":
-                    first = 0 if key == "a03_0" else 2
-                    a_rows[first] = t[:, 0:N_NODES]
-                    a_rows[first + 1] = t[:, N_NODES : 2 * N_NODES]
-            else:
-                m = int(key[1:])
-                t = keep.tile([P, N_NODES], BF16, name="in_" + key)
-                nc.sync.dma_start(out=t[:], in_=adjacency_matrix[P * m : P * (m + 1), :])
-                a_rows[m] = t[:]
-            T[key] = t
+        def load(name, src):
+            width = 1
+            for n in src.shape[1:]:
+                width = width * n
+            t = keep.tile([P, width], BF16, name=name)
+            dst = t[:] if len(src.shape) == 2 else t[:].rearrange("p (a b) -> p a b", a=src.shape[1])
+            nc.sync.dma_start(out=dst, in_=src)
+            return t
 
-        def pairs(dst):
-            return dst[:].bitcast(BF16).rearrange("q (u n e) -> q u n e", u=2, e=2)
+        wg_in = []
+        xl_in = []
+        for i in range(4):
+            wg_in.append(load("wg_in%d" % i, W_gcn[i * P : (i + 1) * P, :]))
+            xl_in.append(load("xl_in%d" % i, x_lo[:, i // 2, i % 2, :]))
+        a_rows = []
+        xh_in = []
+        for u in range(2):
+            t = load("a_lo%d" % u, a_lo[:, u, :, :])
+            a_rows += [t[:, 0:N_NODES], t[:, N_NODES : 2 * N_NODES]]
+            if u == 0:
+                xh_in.append(load("xh_in0", x_hi[:, 0, :, :]))
+        for m in range(4, 8):
+            a_rows.append(load("a_in%d" % m, adjacency_matrix[m * P : (m + 1) * P, :])[:])
+        xh_in.append(load("xh_in1", x_hi[:, 1, :, :]))
+        ws_in = [load("ws_in%d" % i, W_skip[i * 256 : (i + 1) * 256, :].rearrange("(b p) c -> p b c", b=2)) for i in range(2)]
 
-        def t_pair(src, bk):
+        def words_to(name, n):
+            return keep.tile([P, 2 * n], F32, name=name)
+
+        def pairs(t):
+            return t[:].bitcast(BF16).rearrange("q (u n e) -> q u n e", u=2, e=2)
+
+        wgT_w = [words_to("wgT%d" % i, P) for i in range(4)]
+        xlT_w = [words_to("xlT%d" % i, P) for i in range(4)]
+        xhT_w = [words_to("xhT%d" % i, 2 * P) for i in range(2)]
+        wsT_w = words_to("wsT", 4 * P)
+        wgT = [pairs(t) for t in wgT_w]
+        xlT = [pairs(t) for t in xlT_w]
+        xhT = [pairs(t) for t in xhT_w]
+        wsT = pairs(wsT_w)
+
+        def t_words(bk, src, blocks):
             words = src[:].bitcast(F32)
             for u in range(2):
-                for b in range(2):
-                    k = 2 * u + b
-                    nc.tensor.transpose(bk[:, k * P : (k + 1) * P], words[:, b * 256 + u * P : b * 256 + (u + 1) * P], ident_f[:])
+                for b in range(blocks):
+                    k = u * blocks + b
+                    nc.tensor.transpose(bk[:, k * P : (k + 1) * P], words[:, b * 256 + u * P : b * 256 + (u + 1) * P], ident[:])
 
-        def c_pair(bk, key, eng):
-            if key == "ws0" or key == "ws1":
-                b0 = 0 if key == "ws0" else 2
-                dst_v = wsT_w[:].rearrange("q (u n) -> q u n", u=2)[:, :, b0 * P : (b0 + 2) * P]
-                src_v = bk[:].rearrange("q (u n) -> q u n", u=2)
-            else:
-                dst_v = WORDS[key][:]
-                src_v = bk[:]
+        def copy(eng, dst, src):
             if eng == "v":
-                nc.vector.tensor_copy(out=dst_v, in_=src_v)
+                nc.vector.tensor_copy(out=dst, in_=src)
             else:
-                nc.scalar.copy(out=dst_v, in_=src_v)
+                nc.scalar.copy(out=dst, in_=src)
 
         hgrp = [keep.tile([P, 4 * D], BF16, name="hgrp%d" % g, align_bytes=64) for g in range(2)]
         hcodes = [keep.tile([P, D], U32, name="hcodes%d" % g, align_bytes=64) for g in range(2)]
         hscales = [keep.tile([P, D], U8, name="hscales%d" % g, align_bytes=64) for g in range(2)]
 
-        def h_grp(bk, g, t, oc):
-            xt = PAIRS["x%d%d" % (g, t // 2)]
-            wt = PAIRS["wg%d" % (oc // 2)]
-            cols = slice((t % 2) * P, (t % 2 + 1) * P) if g == 0 else slice(t % 2, 2 * P, 2)
+        def h_group(bk, g, t, oc):
             for ci, (u, e) in enumerate(CHUNKS):
                 nc.tensor.matmul(
                     bk[:, t * P : (t + 1) * P],
-                    lhsT=xt[:, u, cols, e],
-                    rhs=wt[:, u, (oc % 2) * P : (oc % 2 + 1) * P, e],
+                    lhsT=xlT[t][:, u, :, e] if g == 0 else xhT[t // 2][:, u, t % 2 : 2 * P : 2, e],
+                    rhs=wgT[oc][:, u, :, e],
                     start=(ci == 0),
                     stop=(ci == 3),
                 )
 
-        def h_out(bk, g, oc, eng):
-            dst_v = hgrp[g][:, oc * 512 : (oc + 1) * 512].rearrange("p (o t) -> p o t", t=4)
-            src_v = bk[:].rearrange("p (t o) -> p o t", t=4)
-            if eng == "v":
-                nc.vector.tensor_copy(out=dst_v, in_=src_v)
-            else:
-                nc.scalar.copy(out=dst_v, in_=src_v)
+        def h_out(eng, bk, g, oc):
+            copy(
+                eng,
+                hgrp[g][:, oc * 512 : (oc + 1) * 512].rearrange("p (o t) -> p o t", t=4),
+                bk[:].rearrange("p (t o) -> p o t", t=4),
+            )
 
         def q_h(g):
             nc.vector.quantize_mx(out=hcodes[g][:].bitcast(FP8X4), scales=hscales[g][:], in_=hgrp[g][:])
 
-        def deg_v(tile_idx, dst):
-            rows = a_rows[tile_idx]
-            junk = scratch.tile([P, 512], F32, name="junk")
-            nc.vector.scalar_tensor_tensor(
-                out=junk[:], in0=rows[:, 0:512], scalar=1.0, in1=rows[:, 512:1024],
-                op0=ALU.mult, op1=ALU.add, accum_out=dst,
-            )
-
-        def deg_f(tile_idx, dst):
-            junk_b = scratch.tile([P, N_NODES], BF16, name="junk_b")
-            nc.vector.tensor_scalar(out=junk_b[:], in0=a_rows[tile_idx], scalar1=1.0, scalar2=None, op0=ALU.mult, op1=ALU.add, accum_out=dst)
-
-        def deg_s(tile_idx, dst):
-            junk_s = scratch.tile([P, N_NODES], BF16, name="junk_s")
-            nc.scalar.activation(out=junk_s[:], in_=a_rows[tile_idx], func=ACT.Copy, accum_out=dst)
-
+        deg = [keep.tile([P, 4], F32, name="deg%d" % h) for h in range(2)]
         rec = [keep.tile([P, 4], F32, name="rec%d" % h) for h in range(2)]
         dcol = [keep.tile([P, 4], F32, name="dcol%d" % h) for h in range(2)]
-        drep = [keep.tile([P, 4 * P], F32, name="drep%d" % h) for h in range(2)]
-        dj = [None, None]
 
-        def d_rep(h):
-            nc.scalar.activation(
-                out=drep[h][:].rearrange("p (k r) -> p k r", k=4),
-                in_=rec[h][:].unsqueeze(2).to_broadcast([P, 4, P]),
-                func=ACT.Sqrt,
-            )
+        def degree(m):
+            junk = scratch.tile([P, N_NODES], BF16, name="junk")
+            nc.vector.tensor_scalar(out=junk[:], in0=a_rows[m], scalar1=1.0, scalar2=None, op0=ALU.mult, op1=ALU.add, accum_out=deg[m // 4][:, m % 4 : m % 4 + 1])
+
+        def d_of(h):
+            nc.vector.tensor_scalar_add(rec[h][:], deg[h][:], 1e-8)
+            nc.vector.reciprocal(rec[h][:], rec[h][:])
+
+        def d_root(h):
             nc.scalar.sqrt(dcol[h][:], rec[h][:])
 
-        def d_sq(h):
-            nc.scalar.sqrt(dcol[h][:], rec[h][:])
-
-        def t_dj(h):
+        def spread_d(bk, h):
             for k in range(4):
-                nc.tensor.transpose(dj[h][:, k * P : (k + 1) * P], dcol[h][:, k : k + 1].to_broadcast([P, P]), ident_f[:])
+                nc.tensor.transpose(bk[:, k * P : (k + 1) * P], dcol[h][:, k : k + 1].to_broadcast([P, P]), ident[:])
 
         ahat = [keep.tile([P, N_NODES], BF16, name="ahat%d" % m) for m in range(6)]
+        agrp = [keep.tile([P, N_NODES], BF16, name="agrp%d" % m, align_bytes=64) for m in range(6)]
+        acodes = [keep.tile([P, 256], U32, name="acodes%d" % m, align_bytes=64) for m in range(6)]
+        ascales = [keep.tile([P, 256], U8, name="ascales%d" % m, align_bytes=64) for m in range(6)]
 
-        def sc(m, g):
-            c = m % 4
+        def scale(m, g):
             for u in range(2):
                 dst = ahat[m][:, g * 512 + u * 256 : g * 512 + (u + 1) * 256]
                 src = a_rows[m][:, g * 512 : (g + 1) * 512]
                 if g == 0:
                     dst_v = dst.rearrange("i (p e) -> i p e", e=2)
                     src_v = src[:, u * 256 : (u + 1) * 256].rearrange("i (p e) -> i p e", e=2)
-                    in1 = dj[0][:, u * 256 : (u + 1) * 256].rearrange("i (e p) -> i p e", e=2)
+                    dj_v = dj[0][:, u * 256 : (u + 1) * 256].rearrange("i (e p) -> i p e", e=2)
                 else:
                     dst_v = dst.rearrange("i (h x) -> i h x", h=2)
                     src_v = src.rearrange("i (h u x) -> i u h x", h=2, u=2)[:, u, :, :]
-                    in1 = dj[1][:].rearrange("i (h u x) -> i u h x", h=2, u=2)[:, u, :, :]
-                nc.vector.scalar_tensor_tensor(
-                    out=dst_v,
-                    in0=src_v,
-                    scalar=dcol[m // 4][:, c : c + 1],
-                    in1=in1,
-                    op0=ALU.mult,
-                    op1=ALU.mult,
-                )
+                    dj_v = dj[1][:].rearrange("i (h u x) -> i u h x", h=2, u=2)[:, u, :, :]
+                nc.vector.scalar_tensor_tensor(out=dst_v, in0=src_v, scalar=dcol[m // 4][:, m % 4 : m % 4 + 1], in1=dj_v, op0=ALU.mult, op1=ALU.mult)
 
-        agrp = [keep.tile([P, N_NODES], BF16, name="agrp%d" % m, align_bytes=64) for m in range(6)]
-        acodes = [keep.tile([P, 256], U32, name="acodes%d" % m, align_bytes=64) for m in range(6)]
-        ascales = [keep.tile([P, 256], U8, name="ascales%d" % m, align_bytes=64) for m in range(6)]
-        skip_sb = [keep.tile([P, D], F32, name="skip%d" % m) for m in range(6)]
-        pre = [keep.tile([P, D], F32, name="pre%d" % m) for m in range(6)]
-        fin = [keep.tile([P, D], F32, name="fin%d" % m) for m in range(6)]
+        def a_word(bk, m, k):
+            nc.tensor.transpose(bk[:, k * P : (k + 1) * P], ahat[m][:].bitcast(F32)[:, k * P : (k + 1) * P], ident[:])
 
-        def at_word(bk, m, b):
-            words = ahat[m][:].bitcast(F32)
-            nc.tensor.transpose(bk[:, b * P : (b + 1) * P], words[:, b * P : (b + 1) * P], ident_f[:])
-
-        def a_out(bk, m, eng):
-            dst_v = agrp[m][:].bitcast(F32).rearrange("p (g i u) -> p g i u", g=2, u=2)
-            src_v = bk[:].rearrange("p (g u i) -> p g i u", g=2, u=2)
-            if eng == "v":
-                nc.vector.tensor_copy(out=dst_v, in_=src_v)
-            else:
-                nc.scalar.copy(out=dst_v, in_=src_v)
+        def a_out(eng, bk, m):
+            copy(eng, agrp[m][:].bitcast(F32).rearrange("p (g i u) -> p g i u", g=2, u=2), bk[:].rearrange("p (g u i) -> p g i u", g=2, u=2))
 
         def q_a(m):
             nc.vector.quantize_mx(out=acodes[m][:].bitcast(FP8X4), scales=ascales[m][:], in_=agrp[m][:])
 
-        def sk_one(bk, m, ci):
-            xt = PAIRS["x0%d" % (m // 2)] if m < 4 else PAIRS["x1%d" % (m - 4)]
-            col = (m % 2) * P if m < 4 else 0
+        skip = [keep.tile([P, D], F32, name="skip%d" % m) for m in range(6)]
+        pre = [keep.tile([P, D], F32, name="pre%d" % m) for m in range(6)]
+        fin = [keep.tile([P, D], F32, name="fin%d" % m) for m in range(6)]
+
+        def skip_mm(bk, m, ci, lo=0, hi=D):
             u, e = CHUNKS[ci]
-            nc.tensor.matmul(bk[:], lhsT=xt[:, u, col : col + P, e], rhs=wsT[:, u, :, e], start=(ci == 0), stop=(ci == 3))
+            lhsT = xlT[m][:, u, :, e] if m < 4 else xhT[m - 4][:, u, 0:P, e]
+            nc.tensor.matmul(bk[:, 0 : hi - lo], lhsT=lhsT, rhs=wsT[:, u, lo:hi, e], start=(ci == 0), stop=(ci == 3))
 
-        def s_out(bk, m):
-            nc.scalar.activation(out=skip_sb[m][:], in_=bk[:], func=ACT.Copy, scale=0.5)
+        def skip_out(bk, m, lo=0, hi=D):
+            nc.scalar.activation(out=skip[m][:, lo:hi], in_=bk[:, 0 : hi - lo], func=ACT.Copy, scale=0.5)
 
-        def mx(bk, m):
+        def mx(bk, m, lo=0, hi=D):
             for g in range(2):
                 nc.tensor.matmul_mx(
-                    out=bk[:],
+                    out=bk[:, 0 : hi - lo],
                     lhsT=acodes[m][:, g * P : (g + 1) * P].bitcast(FP8X4),
                     lhsT_scale=ascales[m][:, g * P : (g + 1) * P],
-                    rhs=hcodes[g][:].bitcast(FP8X4),
-                    rhs_scale=hscales[g][:],
+                    rhs=hcodes[g][:, lo:hi].bitcast(FP8X4),
+                    rhs_scale=hscales[g][:, lo:hi],
                     start=(g == 0),
                     stop=(g == 1),
                 )
 
-        out03 = out[0:512, :].rearrange("(u p e) o -> p u e o", u=2, e=2)
+        def residual(m):
+            return xl_in[m] if m < 4 else xh_in[m - 4]
 
-        def e1(bk, m):
-            nc.vector.scalar_tensor_tensor(out=pre[m][:], in0=bk[:], scalar=0.5, in1=skip_sb[m][:], op0=ALU.mult, op1=ALU.add)
+        def e1(bk, m, lo=0, hi=D):
+            nc.vector.scalar_tensor_tensor(out=pre[m][:, lo:hi], in0=bk[:, 0 : hi - lo], scalar=0.5, in1=skip[m][:, lo:hi], op0=ALU.mult, op1=ALU.add)
 
-        def e2(m):
-            res = T["x0%d" % (m // 2)][:, (m % 2) * D : (m % 2 + 1) * D] if m < 4 else T["x1%d" % (m - 4)][:, 0:D]
-            nc.vector.scalar_tensor_tensor(out=fin[m][:], in0=pre[m][:], scalar=0.0, in1=res, op0=ALU.max, op1=ALU.add)
+        def e2(m, lo=0, hi=D):
+            nc.vector.scalar_tensor_tensor(out=fin[m][:, lo:hi], in0=pre[m][:, lo:hi], scalar=0.0, in1=residual(m)[:, lo:hi], op0=ALU.max, op1=ALU.add)
 
-        def st(m):
-            dst = out03[:, m // 2, m % 2, :] if m < 4 else out[P * m : P * (m + 1), :]
-            nc.sync.dma_start(out=dst, in_=fin[m][:])
+        def store(m, lo=0, hi=D):
+            dst = out_lo[:, m // 2, m % 2, lo:hi] if m < 4 else out[m * P : (m + 1) * P, lo:hi]
+            nc.sync.dma_start(out=dst, in_=fin[m][:, lo:hi])
 
-        wsT_w = keep.tile([P, 8 * P], F32, name="wsT")
-        wsT = pairs(wsT_w)
-        WORDS = {}
-        PAIRS = {}
-        for key in ["wg0", "wg1", "x00", "x01", "x10", "x11"]:
-            WORDS[key] = keep.tile([P, 4 * P], F32, name="w_" + key)
-            PAIRS[key] = pairs(WORDS[key])
-        deg = [keep.tile([P, 4], F32, name="deg%d" % h) for h in range(2)]
+        sides = [(wg_in, wgT_w, "v"), (xl_in, xlT_w, "s")]
 
-        ld("wg0")
-        ld("x00")
-        ld("wg1")
-        ld("x01")
-        ld("a03_0")
-        ld("a03_1")
-        ld("x10")
-        ld("a4")
-        ld("a5")
-        ld("a6")
-        ld("a7")
-        ld("x11")
-        ld("ws0")
-        ld("ws1")
-        k0 = bank(4, F32)
-        t_pair(T["wg0"], k0)
-        k1 = bank(5, F32)
-        t_pair(T["x00"], k1)
-        c_pair(k0, "wg0", "v")
-        k2 = bank(6, F32)
-        t_pair(T["wg1"], k2)
-        c_pair(k1, "x00", "s")
-        k3 = bank(7, F32)
-        t_pair(T["x01"], k3)
-        c_pair(k2, "wg1", "v")
-        k4 = bank(0, F32)
-        h_grp(k4, 0, 0, 0)
-        h_grp(k4, 0, 1, 0)
-        c_pair(k3, "x01", "s")
-        k5 = bank(1, F32)
-        h_grp(k5, 0, 0, 1)
-        h_grp(k5, 0, 1, 1)
-        deg_f(0, deg[0][:, 0:1])
-        k6 = bank(2, F32)
-        h_grp(k6, 0, 0, 2)
-        h_grp(k6, 0, 1, 2)
-        deg_f(1, deg[0][:, 1:2])
-        k7 = bank(3, F32)
-        h_grp(k7, 0, 0, 3)
-        h_grp(k7, 0, 1, 3)
-        deg_f(2, deg[0][:, 2:3])
-        h_grp(k4, 0, 2, 0)
-        h_grp(k4, 0, 3, 0)
-        deg_f(3, deg[0][:, 3:4])
-        nc.vector.tensor_scalar_add(rec[0][:], deg[0][:], 1e-8)
-        nc.vector.reciprocal(rec[0][:], rec[0][:])
-        h_grp(k5, 0, 2, 1)
-        h_grp(k5, 0, 3, 1)
-        d_sq(0)
-        deg_f(4, deg[1][:, 0:1])
-        h_out(k4, 0, 0, "s")
-        k8 = bank(4, F32)
-        t_pair(T["x10"], k8)
-        deg_f(5, deg[1][:, 1:2])
-        dj[0] = bank(5, F32)
-        t_dj(0)
-        h_out(k5, 0, 1, "s")
-        h_grp(k6, 0, 2, 2)
-        h_grp(k6, 0, 3, 2)
-        deg_f(6, deg[1][:, 2:3])
-        c_pair(k8, "x10", "s")
-        h_grp(k7, 0, 2, 3)
-        h_grp(k7, 0, 3, 3)
-        deg_f(7, deg[1][:, 3:4])
-        h_out(k6, 0, 2, "s")
-        k9 = bank(0, F32)
-        h_grp(k9, 1, 0, 0)
-        h_grp(k9, 1, 1, 0)
-        nc.vector.tensor_scalar_add(rec[1][:], deg[1][:], 1e-8)
-        nc.vector.reciprocal(rec[1][:], rec[1][:])
-        sc(0, 0)
-        d_sq(1)
-        h_out(k7, 0, 3, "s")
-        k10 = bank(1, F32)
-        h_grp(k10, 1, 0, 1)
-        h_grp(k10, 1, 1, 1)
-        sc(1, 0)
-        k11 = bank(6, F32)
-        t_pair(T["x11"], k11)
-        sc(2, 0)
-        dj[1] = bank(7, F32)
-        t_dj(1)
-        c_pair(k11, "x11", "s")
-        k12 = bank(2, F32)
-        h_grp(k12, 1, 0, 2)
-        h_grp(k12, 1, 1, 2)
-        sc(3, 0)
-        k13 = bank(3, F32)
-        h_grp(k13, 1, 0, 3)
-        h_grp(k13, 1, 1, 3)
-        sc(0, 1)
-        k14 = bank(4, F32)
-        t_pair(T["ws0"], k14)
-        sc(1, 1)
-        h_grp(k9, 1, 2, 0)
-        h_grp(k9, 1, 3, 0)
-        c_pair(k14, "ws0", "s")
+        def piece(i):
+            src, dst, eng = sides[i % 2]
+            bk = bank(4 + i % 4)
+            t_words(bk, src[i // 2], 1)
+            copy(eng, dst[i // 2][:], bk[:, 0 : 2 * P])
+
+        for i in range(4):
+            piece(i)
+
+        hb = [bank(i) for i in range(4)]
+
+        def h0(t, oc):
+            h_group(hb[oc], 0, t, oc)
+
+        h0(0, 0)
+        h0(0, 1)
+        piece(4)
+        piece(5)
+        h0(1, 0)
+        piece(6)
+        h0(1, 1)
+        piece(7)
+        h0(0, 2)
+        h0(1, 2)
+        degree(0)
+        degree(1)
+        h0(2, 0)
+        h0(2, 1)
+        h0(2, 2)
+        h0(3, 0)
+        h_out("s", hb[0], 0, 0)
+        h0(3, 1)
+        h_out("s", hb[1], 0, 1)
+        degree(2)
+        degree(3)
+        d_of(0)
+        xb = bank(6)
+        t_words(xb, xh_in[0], 2)
+        copy("s", xhT_w[0][:], xb[:])
+        h0(3, 2)
+        d_root(0)
+        h_out("s", hb[2], 0, 2)
+        degree(4)
+        dj = [bank(4), bank(5)]
+        for t in range(4):
+            h0(t, 3)
+        h_out("s", hb[3], 0, 3)
+        degree(5)
+        degree(6)
+        degree(7)
+        d_of(1)
+        d_root(1)
+
+        h1 = [bank(i) for i in range(4)]
+
+        def hx(ts, oc):
+            for t in ts:
+                h_group(h1[oc], 1, t, oc)
+
+        hx([0, 1], 0)
+        spread_d(dj[0], 0)
+        scale(0, 0)
+        hx([0, 1], 1)
+        scale(1, 0)
+        hx([0, 1], 2)
+        xb = bank(7)
+        t_words(xb, xh_in[1], 2)
+        copy("s", xhT_w[1][:], xb[:])
+        scale(2, 0)
+        hx([0, 1], 3)
+        spread_d(dj[1], 1)
+        scale(3, 0)
+        scale(0, 1)
+        wsT_v = wsT_w[:].rearrange("q (u n) -> q u n", u=2)
+
+        def t_ws(i, k):
+            bk = bank(i)
+            t_words(bk, ws_in[k], 2)
+            copy("s", wsT_v[:, :, 2 * k * P : 2 * (k + 1) * P], bk[:].rearrange("q (u n) -> q u n", u=2))
+
+        t_ws(6, 0)
+        scale(1, 1)
+        hx([2, 3], 0)
         q_h(0)
-        k15 = bank(6, F32)
-        t_pair(T["ws1"], k15)
-        h_out(k9, 1, 0, "s")
-        h_grp(k10, 1, 2, 1)
-        h_grp(k10, 1, 3, 1)
-        sc(2, 1)
-        c_pair(k15, "ws1", "s")
-        h_grp(k12, 1, 2, 2)
-        h_grp(k12, 1, 3, 2)
-        sc(3, 1)
-        h_out(k10, 1, 1, "s")
-        h_grp(k13, 1, 2, 3)
-        h_grp(k13, 1, 3, 3)
-        sc(4, 0)
-        h_out(k12, 1, 2, "s")
-        sc(4, 1)
-        k17 = bank(6, F32)
-        at_word(k17, 0, 0)
-        h_out(k13, 1, 3, "s")
-        at_word(k17, 0, 1)
-        at_word(k17, 0, 2)
-        at_word(k17, 0, 3)
-        sc(5, 0)
-        k18 = bank(0, F32)
-        sk_one(k18, 0, 0)
-        sc(5, 1)
-        a_out(k17, 0, "s")
-        k19 = bank(5, F32)
-        at_word(k19, 1, 0)
-        sk_one(k18, 0, 1)
-        at_word(k19, 1, 1)
-        at_word(k19, 1, 2)
-        sk_one(k18, 0, 2)
+        h_out("s", h1[0], 1, 0)
+        t_ws(7, 1)
+        hx([2, 3], 1)
+        scale(2, 1)
+        hx([2, 3], 2)
+        scale(3, 1)
+        h_out("s", h1[1], 1, 1)
+        hx([2, 3], 3)
+        scale(4, 0)
+        h_out("s", h1[2], 1, 2)
+        scale(4, 1)
+        h_out("s", h1[3], 1, 3)
+
+        at_bank = {}
+        sk_bank = {}
+        mx_bank = {}
+
+        def at(m, i):
+            at_bank[m] = bank(i)
+            for k in range(4):
+                a_word(at_bank[m], m, k)
+            a_out("s", at_bank[m], m)
+
+        def sk(m, i, n=None, j=None):
+            sk_bank[m] = bank(i)
+            for ci in range(4):
+                skip_mm(sk_bank[m], m, ci)
+                if ci == 1 and n is not None:
+                    at(n, j)
+
+        def product(m, i):
+            mx_bank[m] = bank(i)
+            mx(mx_bank[m], m)
+
+        at(0, 6)
         q_h(1)
-        at_word(k19, 1, 3)
-        k20 = bank(4, F32)
-        sk_one(k18, 0, 3)
-        at_word(k20, 2, 0)
-        at_word(k20, 2, 1)
-        k21 = bank(1, F32)
-        sk_one(k21, 1, 0)
-        a_out(k19, 1, "s")
+        at(1, 7)
+        sk(0, 0, 2, 1)
         q_a(0)
-        at_word(k20, 2, 2)
-        sk_one(k21, 1, 1)
-        at_word(k20, 2, 3)
-        k22 = bank(7, F32)
-        at_word(k22, 3, 0)
-        sk_one(k21, 1, 2)
-        at_word(k22, 3, 1)
-        sk_one(k21, 1, 3)
-        s_out(k18, 0)
-        at_word(k22, 3, 2)
-        at_word(k22, 3, 3)
-        k23 = bank(2, F32)
-        mx(k23, 0)
+        scale(5, 0)
         q_a(1)
-        a_out(k20, 2, "s")
-        k24 = bank(3, F32)
-        sk_one(k24, 2, 0)
-        k25 = bank(6, F32)
-        at_word(k25, 4, 0)
-        sk_one(k24, 2, 1)
-        at_word(k25, 4, 1)
-        at_word(k25, 4, 2)
-        sk_one(k24, 2, 2)
-        a_out(k22, 3, "s")
-        at_word(k25, 4, 3)
-        k26 = bank(5, F32)
-        sk_one(k24, 2, 3)
+        scale(5, 1)
+        sk(1, 2, 3, 3)
+        skip_out(sk_bank[0], 0)
+        product(0, 6)
+        skip_out(sk_bank[1], 1)
         q_a(2)
-        at_word(k26, 5, 0)
-        at_word(k26, 5, 1)
-        k27 = bank(0, F32)
-        mx(k27, 1)
-        e1(k23, 0)
-        e2(0)
-        s_out(k21, 1)
-        k28 = bank(2, F32)
-        sk_one(k28, 3, 0)
-        at_word(k26, 5, 2)
-        sk_one(k28, 3, 1)
+        product(1, 7)
+        sk(2, 0, 4, 4)
+        e1(mx_bank[0], 0)
         q_a(3)
-        a_out(k25, 4, "s")
-        at_word(k26, 5, 3)
-        st(0)
-        sk_one(k28, 3, 2)
-        e1(k27, 1)
-        sk_one(k28, 3, 3)
-        k29 = bank(1, F32)
-        mx(k29, 2)
+        e1(mx_bank[1], 1)
+        e2(0)
+        store(0)
+        skip_out(sk_bank[2], 2)
         e2(1)
-        s_out(k24, 2)
-        k30 = bank(0, F32)
-        mx(k30, 3)
+        store(1)
+        product(2, 6)
+        sk(3, 1, 5, 5)
         q_a(4)
-        st(1)
-        a_out(k26, 5, "s")
-        k31 = bank(3, F32)
-        sk_one(k31, 4, 0)
-        e1(k29, 2)
-        sk_one(k31, 4, 1)
-        sk_one(k31, 4, 2)
-        e2(2)
-        sk_one(k31, 4, 3)
-        s_out(k28, 3)
-        k32 = bank(1, F32)
-        mx(k32, 4)
+        e1(mx_bank[2], 2)
+        skip_out(sk_bank[3], 3)
+        product(3, 7)
         q_a(5)
-        st(2)
-        s_out(k31, 4)
-        k33 = bank(2, F32)
-        sk_one(k33, 5, 0)
-        e1(k30, 3)
-        sk_one(k33, 5, 1)
-        sk_one(k33, 5, 2)
+        e2(2)
+        store(2)
+        sk(4, 2)
+        e1(mx_bank[3], 3)
+        skip_out(sk_bank[4], 4)
+        product(4, 6)
         e2(3)
-        sk_one(k33, 5, 3)
-        k34 = bank(3, F32)
-        mx(k34, 5)
-        e1(k32, 4)
-        st(3)
-        s_out(k33, 5)
+        store(3)
+        halves = [(0, 256), (256, 512)]
+        sk5 = [bank(0), bank(3)]
+        mx5 = [bank(4), bank(5)]
+        for i, (lo, hi) in enumerate(halves):
+            for ci in range(4):
+                skip_mm(sk5[i], 5, ci, lo, hi)
+            skip_out(sk5[i], 5, lo, hi)
+        for i, (lo, hi) in enumerate(halves):
+            mx(mx5[i], 5, lo, hi)
+        e1(mx_bank[4], 4)
         e2(4)
-        e1(k34, 5)
-        st(4)
-        e2(5)
-        st(5)
+        store(4)
+        for i, (lo, hi) in enumerate(halves):
+            e1(mx5[i], 5, lo, hi)
+        for lo, hi in halves:
+            e2(5, lo, hi)
+            store(5, lo, hi)

@@ -57,12 +57,10 @@ def tile_structureawaregcn_kernel(tc, adjacency_matrix, node_features, W_gcn, W_
             wg_in.append(load("wg_in%d" % i, W_gcn[i * P : (i + 1) * P, :]))
             xl_in.append(load("xl_in%d" % i, x_lo[:, i // 2, i % 2, :]))
         a_rows = []
-        xh_in = []
+        xh_in = [load("xh_in0", x_hi[:, 0, :, :])]
         for u in range(2):
             t = load("a_lo%d" % u, a_lo[:, u, :, :])
             a_rows += [t[:, 0:N_NODES], t[:, N_NODES : 2 * N_NODES]]
-            if u == 0:
-                xh_in.append(load("xh_in0", x_hi[:, 0, :, :]))
         for m in range(4, 8):
             a_rows.append(load("a_in%d" % m, adjacency_matrix[m * P : (m + 1) * P, :])[:])
         xh_in.append(load("xh_in1", x_hi[:, 1, :, :]))
@@ -137,7 +135,11 @@ def tile_structureawaregcn_kernel(tc, adjacency_matrix, node_features, W_gcn, W_
 
         def spread_d(bk, h):
             for k in range(4):
-                nc.tensor.transpose(bk[:, k * P : (k + 1) * P], dcol[h][:, k : k + 1].to_broadcast([P, P]), ident[:])
+                if h == 0:
+                    dst = bk[:, (k // 2) * 256 + k % 2 : (k // 2 + 1) * 256 : 2]
+                else:
+                    dst = bk[:, k * P : (k + 1) * P]
+                nc.tensor.transpose(dst, dcol[h][:, k : k + 1].to_broadcast([P, P]), ident[:])
 
         ahat = [keep.tile([P, N_NODES], BF16, name="ahat%d" % m) for m in range(6)]
         agrp = [keep.tile([P, N_NODES], BF16, name="agrp%d" % m, align_bytes=64) for m in range(6)]
@@ -145,18 +147,21 @@ def tile_structureawaregcn_kernel(tc, adjacency_matrix, node_features, W_gcn, W_
         ascales = [keep.tile([P, 256], U8, name="ascales%d" % m, align_bytes=64) for m in range(6)]
 
         def scale(m, g):
-            for u in range(2):
-                dst = ahat[m][:, g * 512 + u * 256 : g * 512 + (u + 1) * 256]
-                src = a_rows[m][:, g * 512 : (g + 1) * 512]
-                if g == 0:
-                    dst_v = dst.rearrange("i (p e) -> i p e", e=2)
-                    src_v = src[:, u * 256 : (u + 1) * 256].rearrange("i (p e) -> i p e", e=2)
-                    dj_v = dj[0][:, u * 256 : (u + 1) * 256].rearrange("i (e p) -> i p e", e=2)
-                else:
-                    dst_v = dst.rearrange("i (h x) -> i h x", h=2)
-                    src_v = src.rearrange("i (h u x) -> i u h x", h=2, u=2)[:, u, :, :]
-                    dj_v = dj[1][:].rearrange("i (h u x) -> i u h x", h=2, u=2)[:, u, :, :]
-                nc.vector.scalar_tensor_tensor(out=dst_v, in0=src_v, scalar=dcol[m // 4][:, m % 4 : m % 4 + 1], in1=dj_v, op0=ALU.mult, op1=ALU.mult)
+            di = dcol[m // 4][:, m % 4 : m % 4 + 1]
+            dst = ahat[m][:, g * 512 : (g + 1) * 512]
+            src = a_rows[m][:, g * 512 : (g + 1) * 512]
+            if g == 0:
+                nc.vector.scalar_tensor_tensor(out=dst, in0=src, scalar=di, in1=dj[0][:], op0=ALU.mult, op1=ALU.mult)
+            else:
+                for u in range(2):
+                    nc.vector.scalar_tensor_tensor(
+                        out=dst[:, u * 256 : (u + 1) * 256].rearrange("i (h x) -> i h x", h=2),
+                        in0=src.rearrange("i (h u x) -> i u h x", h=2, u=2)[:, u, :, :],
+                        scalar=di,
+                        in1=dj[1][:].rearrange("i (h u x) -> i u h x", h=2, u=2)[:, u, :, :],
+                        op0=ALU.mult,
+                        op1=ALU.mult,
+                    )
 
         def a_word(bk, m, k):
             nc.tensor.transpose(bk[:, k * P : (k + 1) * P], ahat[m][:].bitcast(F32)[:, k * P : (k + 1) * P], ident[:])
@@ -167,7 +172,7 @@ def tile_structureawaregcn_kernel(tc, adjacency_matrix, node_features, W_gcn, W_
         def q_a(m):
             nc.vector.quantize_mx(out=acodes[m][:].bitcast(FP8X4), scales=ascales[m][:], in_=agrp[m][:])
 
-        skip = [keep.tile([P, D], F32, name="skip%d" % m) for m in range(6)]
+        half = [keep.tile([P, D], F32, name="half%d" % m) for m in range(6)]
         pre = [keep.tile([P, D], F32, name="pre%d" % m) for m in range(6)]
         fin = [keep.tile([P, D], F32, name="fin%d" % m) for m in range(6)]
 
@@ -176,8 +181,8 @@ def tile_structureawaregcn_kernel(tc, adjacency_matrix, node_features, W_gcn, W_
             lhsT = xlT[m][:, u, :, e] if m < 4 else xhT[m - 4][:, u, 0:P, e]
             nc.tensor.matmul(bk[:, 0 : hi - lo], lhsT=lhsT, rhs=wsT[:, u, lo:hi, e], start=(ci == 0), stop=(ci == 3))
 
-        def skip_out(bk, m, lo=0, hi=D):
-            nc.scalar.activation(out=skip[m][:, lo:hi], in_=bk[:, 0 : hi - lo], func=ACT.Copy, scale=0.5)
+        def half_out(bk, m, lo=0, hi=D):
+            nc.scalar.activation(out=half[m][:, lo:hi], in_=bk, func=ACT.Copy, scale=0.5)
 
         def mx(bk, m, lo=0, hi=D):
             for g in range(2):
@@ -195,7 +200,7 @@ def tile_structureawaregcn_kernel(tc, adjacency_matrix, node_features, W_gcn, W_
             return xl_in[m] if m < 4 else xh_in[m - 4]
 
         def e1(bk, m, lo=0, hi=D):
-            nc.vector.scalar_tensor_tensor(out=pre[m][:, lo:hi], in0=bk[:, 0 : hi - lo], scalar=0.5, in1=skip[m][:, lo:hi], op0=ALU.mult, op1=ALU.add)
+            nc.vector.scalar_tensor_tensor(out=pre[m][:, lo:hi], in0=bk, scalar=0.5, in1=half[m][:, lo:hi], op0=ALU.mult, op1=ALU.add)
 
         def e2(m, lo=0, hi=D):
             nc.vector.scalar_tensor_tensor(out=fin[m][:, lo:hi], in0=pre[m][:, lo:hi], scalar=0.0, in1=residual(m)[:, lo:hi], op0=ALU.max, op1=ALU.add)
@@ -210,7 +215,8 @@ def tile_structureawaregcn_kernel(tc, adjacency_matrix, node_features, W_gcn, W_
             src, dst, eng = sides[i % 2]
             bk = bank(4 + i % 4)
             t_words(bk, src[i // 2], 1)
-            copy(eng, dst[i // 2][:], bk[:, 0 : 2 * P])
+            for u in range(2):
+                copy(eng, dst[i // 2][:, u * P : (u + 1) * P], bk[:, u * P : (u + 1) * P])
 
         for i in range(4):
             piece(i)
@@ -235,6 +241,9 @@ def tile_structureawaregcn_kernel(tc, adjacency_matrix, node_features, W_gcn, W_
         h0(2, 0)
         h0(2, 1)
         h0(2, 2)
+        xb = bank(6)
+        t_words(xb, xh_in[0], 2)
+        copy("s", xhT_w[0][:], xb[:])
         h0(3, 0)
         h_out("s", hb[0], 0, 0)
         h0(3, 1)
@@ -242,9 +251,6 @@ def tile_structureawaregcn_kernel(tc, adjacency_matrix, node_features, W_gcn, W_
         degree(2)
         degree(3)
         d_of(0)
-        xb = bank(6)
-        t_words(xb, xh_in[0], 2)
-        copy("s", xhT_w[0][:], xb[:])
         h0(3, 2)
         d_root(0)
         h_out("s", hb[2], 0, 2)
@@ -333,49 +339,63 @@ def tile_structureawaregcn_kernel(tc, adjacency_matrix, node_features, W_gcn, W_
         q_a(1)
         scale(5, 1)
         sk(1, 2, 3, 3)
-        skip_out(sk_bank[0], 0)
+        half_out(sk_bank[0][:], 0)
         product(0, 6)
-        skip_out(sk_bank[1], 1)
+        half_out(sk_bank[1][:], 1)
         q_a(2)
         product(1, 7)
         sk(2, 0, 4, 4)
-        e1(mx_bank[0], 0)
+        e1(mx_bank[0][:], 0)
         q_a(3)
-        e1(mx_bank[1], 1)
+        e1(mx_bank[1][:], 1)
         e2(0)
         store(0)
-        skip_out(sk_bank[2], 2)
+        half_out(sk_bank[2][:], 2)
         e2(1)
         store(1)
         product(2, 6)
         sk(3, 1, 5, 5)
         q_a(4)
-        e1(mx_bank[2], 2)
-        skip_out(sk_bank[3], 3)
+        halves = [(0, 256), (256, 512)]
+
+        def epilogue(m):
+            for lo, hi in halves:
+                e1(mx_bank[m][:, lo:hi], m, lo, hi)
+            for lo, hi in halves:
+                e2(m, lo, hi)
+            store(m)
+
+        epilogue(2)
+        half_out(sk_bank[3][:], 3)
         product(3, 7)
         q_a(5)
-        e2(2)
-        store(2)
         sk(4, 2)
-        e1(mx_bank[3], 3)
-        skip_out(sk_bank[4], 4)
+        epilogue(3)
+        for lo, hi in halves:
+            half_out(sk_bank[4][:, lo:hi], 4, lo, hi)
         product(4, 6)
-        e2(3)
-        store(3)
-        halves = [(0, 256), (256, 512)]
-        sk5 = [bank(0), bank(3)]
-        mx5 = [bank(4), bank(5)]
-        for i, (lo, hi) in enumerate(halves):
+        product(5, 4)
+        for lo, hi in halves:
+            half_out(mx_bank[5][:, lo:hi], 5, lo, hi)
+        epilogue(4)
+        parts = [(0, 256), (256, 384), (384, 512)]
+        sk5 = [bank(0), bank(3), bank(5)]
+        for i, (lo, hi) in enumerate(parts):
             for ci in range(4):
                 skip_mm(sk5[i], 5, ci, lo, hi)
-            skip_out(sk5[i], 5, lo, hi)
-        for i, (lo, hi) in enumerate(halves):
-            mx(mx5[i], 5, lo, hi)
-        e1(mx_bank[4], 4)
-        e2(4)
-        store(4)
-        for i, (lo, hi) in enumerate(halves):
-            e1(mx5[i], 5, lo, hi)
-        for lo, hi in halves:
+
+        def last1(i):
+            lo, hi = parts[i]
+            e1(sk5[i][:, 0 : hi - lo], 5, lo, hi)
+
+        def last2(i):
+            lo, hi = parts[i]
             e2(5, lo, hi)
             store(5, lo, hi)
+
+        last1(0)
+        last1(1)
+        last2(0)
+        last1(2)
+        last2(1)
+        last2(2)

@@ -49,20 +49,24 @@ def tile_structureawaregcn_kernel(tc, adjacency_matrix, node_features, W_gcn, W_
             t = keep.tile([P, width], BF16, name=name)
             dst = t[:] if len(src.shape) == 2 else t[:].rearrange("p (a b) -> p a b", a=src.shape[1])
             nc.sync.dma_start(out=dst, in_=src)
-            return t
+            return t[:]
 
         wg_in = []
         xl_in = []
-        for i in range(4):
+        for i in range(2):
             wg_in.append(load("wg_in%d" % i, W_gcn[i * P : (i + 1) * P, :]))
-            xl_in.append(load("xl_in%d" % i, x_lo[:, i // 2, i % 2, :]))
+            xl_in.append(load("xl_in%d" % i, x_lo[:, 0, i, :]))
+        t = load("wg_in2", W_gcn[2 * P : 4 * P, :].rearrange("(b p) c -> p b c", b=2))
+        wg_in += [t[:, 0:D], t[:, D : 2 * D]]
+        t = load("xl_in2", x_lo[:, 1, :, :])
+        xl_in += [t[:, 0:D], t[:, D : 2 * D]]
         a_rows = []
         xh_in = [load("xh_in0", x_hi[:, 0, :, :])]
         for u in range(2):
             t = load("a_lo%d" % u, a_lo[:, u, :, :])
             a_rows += [t[:, 0:N_NODES], t[:, N_NODES : 2 * N_NODES]]
         for m in range(4, 8):
-            a_rows.append(load("a_in%d" % m, adjacency_matrix[m * P : (m + 1) * P, :])[:])
+            a_rows.append(load("a_in%d" % m, adjacency_matrix[m * P : (m + 1) * P, :]))
         xh_in.append(load("xh_in1", x_hi[:, 1, :, :]))
         ws_in = [load("ws_in%d" % i, W_skip[i * 256 : (i + 1) * 256, :].rearrange("(b p) c -> p b c", b=2)) for i in range(2)]
 
@@ -82,7 +86,7 @@ def tile_structureawaregcn_kernel(tc, adjacency_matrix, node_features, W_gcn, W_
         wsT = pairs(wsT_w)
 
         def t_words(bk, src, blocks):
-            words = src[:].bitcast(F32)
+            words = src.bitcast(F32)
             for u in range(2):
                 for b in range(blocks):
                     k = u * blocks + b
@@ -126,8 +130,10 @@ def tile_structureawaregcn_kernel(tc, adjacency_matrix, node_features, W_gcn, W_
             junk = scratch.tile([P, N_NODES], BF16, name="junk")
             nc.vector.tensor_scalar(out=junk[:], in0=a_rows[m], scalar1=1.0, scalar2=None, op0=ALU.mult, op1=ALU.add, accum_out=deg[m // 4][:, m % 4 : m % 4 + 1])
 
-        def d_of(h):
+        def d_add(h):
             nc.vector.tensor_scalar_add(rec[h][:], deg[h][:], 1e-8)
+
+        def d_reciprocal(h):
             nc.vector.reciprocal(rec[h][:], rec[h][:])
 
         def d_root(h):
@@ -229,11 +235,11 @@ def tile_structureawaregcn_kernel(tc, adjacency_matrix, node_features, W_gcn, W_
         h0(0, 0)
         h0(0, 1)
         piece(4)
-        piece(5)
-        h0(1, 0)
         piece(6)
-        h0(1, 1)
+        h0(1, 0)
+        piece(5)
         piece(7)
+        h0(1, 1)
         h0(0, 2)
         h0(1, 2)
         degree(0)
@@ -250,7 +256,8 @@ def tile_structureawaregcn_kernel(tc, adjacency_matrix, node_features, W_gcn, W_
         h_out("s", hb[1], 0, 1)
         degree(2)
         degree(3)
-        d_of(0)
+        d_add(0)
+        d_reciprocal(0)
         h0(3, 2)
         d_root(0)
         h_out("s", hb[2], 0, 2)
@@ -262,8 +269,6 @@ def tile_structureawaregcn_kernel(tc, adjacency_matrix, node_features, W_gcn, W_
         degree(5)
         degree(6)
         degree(7)
-        d_of(1)
-        d_root(1)
 
         h1 = [bank(i) for i in range(4)]
 
@@ -273,9 +278,12 @@ def tile_structureawaregcn_kernel(tc, adjacency_matrix, node_features, W_gcn, W_
 
         hx([0, 1], 0)
         spread_d(dj[0], 0)
+        d_add(1)
         scale(0, 0)
         hx([0, 1], 1)
+        d_reciprocal(1)
         scale(1, 0)
+        d_root(1)
         hx([0, 1], 2)
         xb = bank(7)
         t_words(xb, xh_in[1], 2)

@@ -55,7 +55,9 @@ def tile_structureawaregcn_kernel(tc, adjacency_matrix, node_features, W_gcn, W_
         xl_in = []
         for i in range(2):
             wg_in.append(load("wg_in%d" % i, W_gcn[i * P : (i + 1) * P, :]))
-            xl_in.append(load("xl_in%d" % i, x_lo[:, 0, i, :]))
+            if i == 0:
+                t = load("xl_in0", x_lo[:, 0, :, :])
+                xl_in += [t[:, 0:D], t[:, D : 2 * D]]
         t = load("wg_in2", W_gcn[2 * P : 4 * P, :].rearrange("(b p) c -> p b c", b=2))
         wg_in += [t[:, 0:D], t[:, D : 2 * D]]
         t = load("xl_in2", x_lo[:, 1, :, :])
@@ -65,7 +67,9 @@ def tile_structureawaregcn_kernel(tc, adjacency_matrix, node_features, W_gcn, W_
         for u in range(2):
             t = load("a_lo%d" % u, a_lo[:, u, :, :])
             a_rows += [t[:, 0:N_NODES], t[:, N_NODES : 2 * N_NODES]]
-        for m in range(4, 8):
+        t = load("a_in4", adjacency_matrix[4 * P : 6 * P, :].rearrange("(b p) j -> p b j", b=2))
+        a_rows += [t[:, 0:N_NODES], t[:, N_NODES : 2 * N_NODES]]
+        for m in range(6, 8):
             a_rows.append(load("a_in%d" % m, adjacency_matrix[m * P : (m + 1) * P, :]))
         xh_in.append(load("xh_in1", x_hi[:, 1, :, :]))
         ws_in = [load("ws_in%d" % i, W_skip[i * 256 : (i + 1) * 256, :].rearrange("(b p) c -> p b c", b=2)) for i in range(2)]
@@ -152,12 +156,14 @@ def tile_structureawaregcn_kernel(tc, adjacency_matrix, node_features, W_gcn, W_
         acodes = [keep.tile([P, 256], U32, name="acodes%d" % m, align_bytes=64) for m in range(6)]
         ascales = [keep.tile([P, 256], U8, name="ascales%d" % m, align_bytes=64) for m in range(6)]
 
-        def scale(m, g):
+        def scale(m, g, lo=0, hi=512):
             di = dcol[m // 4][:, m % 4 : m % 4 + 1]
             dst = ahat[m][:, g * 512 : (g + 1) * 512]
             src = a_rows[m][:, g * 512 : (g + 1) * 512]
             if g == 0:
-                nc.vector.scalar_tensor_tensor(out=dst, in0=src, scalar=di, in1=dj[0][:], op0=ALU.mult, op1=ALU.mult)
+                nc.vector.scalar_tensor_tensor(
+                    out=dst[:, lo:hi], in0=src[:, lo:hi], scalar=di, in1=dj[0][:, lo:hi], op0=ALU.mult, op1=ALU.mult
+                )
             else:
                 for u in range(2):
                     nc.vector.scalar_tensor_tensor(
@@ -224,7 +230,7 @@ def tile_structureawaregcn_kernel(tc, adjacency_matrix, node_features, W_gcn, W_
             for u in range(2):
                 copy(eng, dst[i // 2][:, u * P : (u + 1) * P], bk[:, u * P : (u + 1) * P])
 
-        for i in range(4):
+        for i in [0, 1, 3, 2]:
             piece(i)
 
         hb = [bank(i) for i in range(4)]
@@ -233,13 +239,13 @@ def tile_structureawaregcn_kernel(tc, adjacency_matrix, node_features, W_gcn, W_
             h_group(hb[oc], 0, t, oc)
 
         h0(0, 0)
-        h0(0, 1)
-        piece(4)
-        piece(6)
         h0(1, 0)
+        piece(4)
+        h0(0, 1)
+        piece(6)
+        h0(1, 1)
         piece(5)
         piece(7)
-        h0(1, 1)
         h0(0, 2)
         h0(1, 2)
         degree(0)
@@ -252,14 +258,14 @@ def tile_structureawaregcn_kernel(tc, adjacency_matrix, node_features, W_gcn, W_
         copy("s", xhT_w[0][:], xb[:])
         h0(3, 0)
         h_out("s", hb[0], 0, 0)
-        h0(3, 1)
-        h_out("s", hb[1], 0, 1)
         degree(2)
         degree(3)
         d_add(0)
         d_reciprocal(0)
-        h0(3, 2)
         d_root(0)
+        h0(3, 1)
+        h_out("s", hb[1], 0, 1)
+        h0(3, 2)
         h_out("s", hb[2], 0, 2)
         degree(4)
         dj = [bank(4), bank(5)]
@@ -278,20 +284,21 @@ def tile_structureawaregcn_kernel(tc, adjacency_matrix, node_features, W_gcn, W_
 
         hx([0, 1], 0)
         spread_d(dj[0], 0)
+        scale(0, 0, 0, 256)
         d_add(1)
-        scale(0, 0)
-        hx([0, 1], 1)
+        scale(0, 0, 256, 512)
         d_reciprocal(1)
-        scale(1, 0)
         d_root(1)
+        scale(1, 0)
+        hx([0, 1], 1)
+        scale(2, 0)
         hx([0, 1], 2)
         xb = bank(7)
         t_words(xb, xh_in[1], 2)
         copy("s", xhT_w[1][:], xb[:])
-        scale(2, 0)
+        scale(3, 0)
         hx([0, 1], 3)
         spread_d(dj[1], 1)
-        scale(3, 0)
         scale(0, 1)
         wsT_v = wsT_w[:].rearrange("q (u n) -> q u n", u=2)
 

from contextlib import ExitStack

import concourse.mybir as mybir
from concourse.masks import make_identity

F32 = mybir.dt.float32
BF16 = mybir.dt.bfloat16
U32 = mybir.dt.uint32
U8 = mybir.dt.uint8
FP8X4 = mybir.dt.float8_e4m3fn_x4
ALU = mybir.AluOpType
ACT = mybir.ActivationFunctionType

P = 128
N_NODES = 1024
D = 512
B = 768
FLOPS = 2 * (B * N_NODES * D + N_NODES * D * D + B * D * D)
CHUNKS = [(0, 0), (0, 1), (1, 0), (1, 1)]


def tile_structureawaregcn_kernel(tc, adjacency_matrix, node_features, W_gcn, W_skip, batch_size, out):
    nc = tc.nc
    assert batch_size == B
    with ExitStack() as ctx:
        keep = ctx.enter_context(tc.tile_pool(name="keep", bufs=1))
        scratch = ctx.enter_context(tc.tile_pool(name="scratch", bufs=2))
        psum = ctx.enter_context(tc.psum_pool(name="psum", bufs=1))
        ctx.enter_context(tc.manual_schedule())

        def bank(i):
            return psum.tile([P, 512], F32, name="bk%d" % i, tag="bk%d" % i)

        warm = keep.tile([P, 1], F32, name="warm")
        nc.vector.memset(warm[:], 1.0)
        nc.scalar.sqrt(warm[:], warm[:])
        ident = keep.tile([P, P], F32, name="ident")
        make_identity(nc, ident[:])

        x_lo = node_features[0:512, :].rearrange("(u p e) c -> p u e c", u=2, e=2)
        x_hi = node_features[512:1024, :].rearrange("(h u p) c -> p u h c", h=2, u=2)
        a_lo = adjacency_matrix[0:512, :].rearrange("(u p e) j -> p u e j", u=2, e=2)
        out_lo = out[0:512, :].rearrange("(u p e) o -> p u e o", u=2, e=2)

        def load(name, src):
            width = 1
            for n in src.shape[1:]:
                width = width * n
            t = keep.tile([P, width], BF16, name=name)
            dst = t[:] if len(src.shape) == 2 else t[:].rearrange("p (a b) -> p a b", a=src.shape[1])
            nc.sync.dma_start(out=dst, in_=src)
            return t[:]

        wg_in = []
        xl_in = []
        for i in range(2):
            wg_in.append(load("wg_in%d" % i, W_gcn[i * P : (i + 1) * P, :]))
            if i == 0:
                t = load("xl_in0", x_lo[:, 0, :, :])
                xl_in += [t[:, 0:D], t[:, D : 2 * D]]
        t = load("wg_in2", W_gcn[2 * P : 4 * P, :].rearrange("(b p) c -> p b c", b=2))
        wg_in += [t[:, 0:D], t[:, D : 2 * D]]
        t = load("xl_in2", x_lo[:, 1, :, :])
        xl_in += [t[:, 0:D], t[:, D : 2 * D]]
        a_rows = []
        xh_in = [load("xh_in0", x_hi[:, 0, :, :])]
        for u in range(2):
            t = load("a_lo%d" % u, a_lo[:, u, :, :])
            a_rows += [t[:, 0:N_NODES], t[:, N_NODES : 2 * N_NODES]]
        t = load("a_in4", adjacency_matrix[4 * P : 6 * P, :].rearrange("(b p) j -> p b j", b=2))
        a_rows += [t[:, 0:N_NODES], t[:, N_NODES : 2 * N_NODES]]
        for m in range(6, 8):
            a_rows.append(load("a_in%d" % m, adjacency_matrix[m * P : (m + 1) * P, :]))
        xh_in.append(load("xh_in1", x_hi[:, 1, :, :]))
        ws_in = [load("ws_in%d" % i, W_skip[i * 256 : (i + 1) * 256, :].rearrange("(b p) c -> p b c", b=2)) for i in range(2)]

        def words_to(name, n):
            return keep.tile([P, 2 * n], F32, name=name)

        def pairs(t):
            return t[:].bitcast(BF16).rearrange("q (u n e) -> q u n e", u=2, e=2)

        wgT_w = [words_to("wgT%d" % i, P) for i in range(4)]
        xlT_w = [words_to("xlT%d" % i, P) for i in range(4)]
        xhT_w = [words_to("xhT%d" % i, 2 * P) for i in range(2)]
        wsT_w = words_to("wsT", 4 * P)
        wgT = [pairs(t) for t in wgT_w]
        xlT = [pairs(t) for t in xlT_w]
        xhT = [pairs(t) for t in xhT_w]
        wsT = pairs(wsT_w)

        def t_words(bk, src, blocks):
            words = src.bitcast(F32)
            for u in range(2):
                for b in range(blocks):
                    k = u * blocks + b
                    nc.tensor.transpose(bk[:, k * P : (k + 1) * P], words[:, b * 256 + u * P : b * 256 + (u + 1) * P], ident[:])

        def copy(eng, dst, src):
            if eng == "v":
                nc.vector.tensor_copy(out=dst, in_=src)
            else:
                nc.scalar.copy(out=dst, in_=src)

        hgrp = [keep.tile([P, 4 * D], BF16, name="hgrp%d" % g, align_bytes=64) for g in range(2)]
        hcodes = [keep.tile([P, D], U32, name="hcodes%d" % g, align_bytes=64) for g in range(2)]
        hscales = [keep.tile([P, D], U8, name="hscales%d" % g, align_bytes=64) for g in range(2)]

        def h_group(bk, g, t, oc):
            for ci, (u, e) in enumerate(CHUNKS):
                nc.tensor.matmul(
                    bk[:, t * P : (t + 1) * P],
                    lhsT=xlT[t][:, u, :, e] if g == 0 else xhT[t // 2][:, u, t % 2 : 2 * P : 2, e],
                    rhs=wgT[oc][:, u, :, e],
                    start=(ci == 0),
                    stop=(ci == 3),
                )

        def h_out(eng, bk, g, oc):
            copy(
                eng,
                hgrp[g][:, oc * 512 : (oc + 1) * 512].rearrange("p (o t) -> p o t", t=4),
                bk[:].rearrange("p (t o) -> p o t", t=4),
            )

        def q_h(g):
            nc.vector.quantize_mx(out=hcodes[g][:].bitcast(FP8X4), scales=hscales[g][:], in_=hgrp[g][:])

        deg = [keep.tile([P, 4], F32, name="deg%d" % h) for h in range(2)]
        rec = [keep.tile([P, 4], F32, name="rec%d" % h) for h in range(2)]
        dcol = [keep.tile([P, 4], F32, name="dcol%d" % h) for h in range(2)]

        def degree(m):
            junk = scratch.tile([P, N_NODES], BF16, name="junk")
            nc.vector.tensor_scalar(out=junk[:], in0=a_rows[m], scalar1=1.0, scalar2=None, op0=ALU.mult, op1=ALU.add, accum_out=deg[m // 4][:, m % 4 : m % 4 + 1])

        def d_add(h):
            nc.vector.tensor_scalar_add(rec[h][:], deg[h][:], 1e-8)

        def d_reciprocal(h):
            nc.vector.reciprocal(rec[h][:], rec[h][:])

        def d_root(h):
            nc.scalar.sqrt(dcol[h][:], rec[h][:])

        def spread_d(bk, h):
            for k in range(4):
                if h == 0:
                    dst = bk[:, (k // 2) * 256 + k % 2 : (k // 2 + 1) * 256 : 2]
                else:
                    dst = bk[:, k * P : (k + 1) * P]
                nc.tensor.transpose(dst, dcol[h][:, k : k + 1].to_broadcast([P, P]), ident[:])

        ahat = [keep.tile([P, N_NODES], BF16, name="ahat%d" % m) for m in range(6)]
        agrp = [keep.tile([P, N_NODES], BF16, name="agrp%d" % m, align_bytes=64) for m in range(6)]
        acodes = [keep.tile([P, 256], U32, name="acodes%d" % m, align_bytes=64) for m in range(6)]
        ascales = [keep.tile([P, 256], U8, name="ascales%d" % m, align_bytes=64) for m in range(6)]

        def scale(m, g, lo=0, hi=512):
            di = dcol[m // 4][:, m % 4 : m % 4 + 1]
            dst = ahat[m][:, g * 512 : (g + 1) * 512]
            src = a_rows[m][:, g * 512 : (g + 1) * 512]
            if g == 0:
                nc.vector.scalar_tensor_tensor(
                    out=dst[:, lo:hi], in0=src[:, lo:hi], scalar=di, in1=dj[0][:, lo:hi], op0=ALU.mult, op1=ALU.mult
                )
            else:
                for u in range(2):
                    nc.vector.scalar_tensor_tensor(
                        out=dst[:, u * 256 : (u + 1) * 256].rearrange("i (h x) -> i h x", h=2),
                        in0=src.rearrange("i (h u x) -> i u h x", h=2, u=2)[:, u, :, :],
                        scalar=di,
                        in1=dj[1][:].rearrange("i (h u x) -> i u h x", h=2, u=2)[:, u, :, :],
                        op0=ALU.mult,
                        op1=ALU.mult,
                    )

        def a_word(bk, m, k):
            nc.tensor.transpose(bk[:, k * P : (k + 1) * P], ahat[m][:].bitcast(F32)[:, k * P : (k + 1) * P], ident[:])

        def a_out(eng, bk, m):
            copy(eng, agrp[m][:].bitcast(F32).rearrange("p (g i u) -> p g i u", g=2, u=2), bk[:].rearrange("p (g u i) -> p g i u", g=2, u=2))

        def q_a(m):
            nc.vector.quantize_mx(out=acodes[m][:].bitcast(FP8X4), scales=ascales[m][:], in_=agrp[m][:])

        half = [keep.tile([P, D], F32, name="half%d" % m) for m in range(6)]
        pre = [keep.tile([P, D], F32, name="pre%d" % m) for m in range(6)]
        fin = [keep.tile([P, D], F32, name="fin%d" % m) for m in range(6)]

        def skip_mm(bk, m, ci, lo=0, hi=D):
            u, e = CHUNKS[ci]
            lhsT = xlT[m][:, u, :, e] if m < 4 else xhT[m - 4][:, u, 0:P, e]
            nc.tensor.matmul(bk[:, 0 : hi - lo], lhsT=lhsT, rhs=wsT[:, u, lo:hi, e], start=(ci == 0), stop=(ci == 3))

        def half_out(bk, m, lo=0, hi=D):
            nc.scalar.activation(out=half[m][:, lo:hi], in_=bk, func=ACT.Copy, scale=0.5)

        def mx(bk, m, lo=0, hi=D):
            for g in range(2):
                nc.tensor.matmul_mx(
                    out=bk[:, 0 : hi - lo],
                    lhsT=acodes[m][:, g * P : (g + 1) * P].bitcast(FP8X4),
                    lhsT_scale=ascales[m][:, g * P : (g + 1) * P],
                    rhs=hcodes[g][:, lo:hi].bitcast(FP8X4),
                    rhs_scale=hscales[g][:, lo:hi],
                    start=(g == 0),
                    stop=(g == 1),
                )

        def residual(m):
            return xl_in[m] if m < 4 else xh_in[m - 4]

        def e1(bk, m, lo=0, hi=D):
            nc.vector.scalar_tensor_tensor(out=pre[m][:, lo:hi], in0=bk, scalar=0.5, in1=half[m][:, lo:hi], op0=ALU.mult, op1=ALU.add)

        def e2(m, lo=0, hi=D):
            nc.vector.scalar_tensor_tensor(out=fin[m][:, lo:hi], in0=pre[m][:, lo:hi], scalar=0.0, in1=residual(m)[:, lo:hi], op0=ALU.max, op1=ALU.add)

        def store(m, lo=0, hi=D):
            dst = out_lo[:, m // 2, m % 2, lo:hi] if m < 4 else out[m * P : (m + 1) * P, lo:hi]
            nc.sync.dma_start(out=dst, in_=fin[m][:, lo:hi])

        sides = [(wg_in, wgT_w, "v"), (xl_in, xlT_w, "s")]

        def piece(i):
            src, dst, eng = sides[i % 2]
            bk = bank(4 + i % 4)
            t_words(bk, src[i // 2], 1)
            for u in range(2):
                copy(eng, dst[i // 2][:, u * P : (u + 1) * P], bk[:, u * P : (u + 1) * P])

        for i in [0, 1, 3, 2]:
            piece(i)

        hb = [bank(i) for i in range(4)]

        def h0(t, oc):
            h_group(hb[oc], 0, t, oc)

        h0(0, 0)
        h0(1, 0)
        piece(4)
        h0(0, 1)
        piece(6)
        h0(1, 1)
        piece(5)
        piece(7)
        h0(0, 2)
        h0(1, 2)
        degree(0)
        degree(1)
        h0(2, 0)
        h0(2, 1)
        h0(2, 2)
        xb = bank(6)
        t_words(xb, xh_in[0], 2)
        copy("s", xhT_w[0][:], xb[:])
        h0(3, 0)
        h_out("s", hb[0], 0, 0)
        degree(2)
        degree(3)
        d_add(0)
        d_reciprocal(0)
        d_root(0)
        h0(3, 1)
        h_out("s", hb[1], 0, 1)
        h0(3, 2)
        h_out("s", hb[2], 0, 2)
        degree(4)
        dj = [bank(4), bank(5)]
        for t in range(4):
            h0(t, 3)
        h_out("s", hb[3], 0, 3)
        degree(5)
        degree(6)
        degree(7)

        h1 = [bank(i) for i in range(4)]

        def hx(ts, oc):
            for t in ts:
                h_group(h1[oc], 1, t, oc)

        hx([0, 1], 0)
        spread_d(dj[0], 0)
        scale(0, 0, 0, 256)
        d_add(1)
        scale(0, 0, 256, 512)
        d_reciprocal(1)
        d_root(1)
        scale(1, 0)
        hx([0, 1], 1)
        scale(2, 0)
        hx([0, 1], 2)
        xb = bank(7)
        t_words(xb, xh_in[1], 2)
        copy("s", xhT_w[1][:], xb[:])
        scale(3, 0)
        hx([0, 1], 3)
        spread_d(dj[1], 1)
        scale(0, 1)
        wsT_v = wsT_w[:].rearrange("q (u n) -> q u n", u=2)

        def t_ws(i, k):
            bk = bank(i)
            t_words(bk, ws_in[k], 2)
            copy("s", wsT_v[:, :, 2 * k * P : 2 * (k + 1) * P], bk[:].rearrange("q (u n) -> q u n", u=2))

        t_ws(6, 0)
        scale(1, 1)
        hx([2, 3], 0)
        q_h(0)
        h_out("s", h1[0], 1, 0)
        t_ws(7, 1)
        hx([2, 3], 1)
        scale(2, 1)
        hx([2, 3], 2)
        scale(3, 1)
        h_out("s", h1[1], 1, 1)
        hx([2, 3], 3)
        scale(4, 0)
        h_out("s", h1[2], 1, 2)
        scale(4, 1)
        h_out("s", h1[3], 1, 3)

        at_bank = {}
        sk_bank = {}
        mx_bank = {}

        def at(m, i):
            at_bank[m] = bank(i)
            for k in range(4):
                a_word(at_bank[m], m, k)
            a_out("s", at_bank[m], m)

        def sk(m, i, n=None, j=None):
            sk_bank[m] = bank(i)
            for ci in range(4):
                skip_mm(sk_bank[m], m, ci)
                if ci == 1 and n is not None:
                    at(n, j)

        def product(m, i):
            mx_bank[m] = bank(i)
            mx(mx_bank[m], m)

        at(0, 6)
        q_h(1)
        at(1, 7)
        sk(0, 0, 2, 1)
        q_a(0)
        scale(5, 0)
        q_a(1)
        scale(5, 1)
        sk(1, 2, 3, 3)
        half_out(sk_bank[0][:], 0)
        product(0, 6)
        half_out(sk_bank[1][:], 1)
        q_a(2)
        product(1, 7)
        sk(2, 0, 4, 4)
        e1(mx_bank[0][:], 0)
        q_a(3)
        e1(mx_bank[1][:], 1)
        e2(0)
        store(0)
        half_out(sk_bank[2][:], 2)
        e2(1)
        store(1)
        product(2, 6)
        sk(3, 1, 5, 5)
        q_a(4)
        halves = [(0, 256), (256, 512)]

        def epilogue(m):
            for lo, hi in halves:
                e1(mx_bank[m][:, lo:hi], m, lo, hi)
            for lo, hi in halves:
                e2(m, lo, hi)
            store(m)

        epilogue(2)
        half_out(sk_bank[3][:], 3)
        product(3, 7)
        q_a(5)
        sk(4, 2)
        epilogue(3)
        for lo, hi in halves:
            half_out(sk_bank[4][:, lo:hi], 4, lo, hi)
        product(4, 6)
        product(5, 4)
        for lo, hi in halves:
            half_out(mx_bank[5][:, lo:hi], 5, lo, hi)
        epilogue(4)
        parts = [(0, 256), (256, 384), (384, 512)]
        sk5 = [bank(0), bank(3), bank(5)]
        for i, (lo, hi) in enumerate(parts):
            for ci in range(4):
                skip_mm(sk5[i], 5, ci, lo, hi)

        def last1(i):
            lo, hi = parts[i]
            e1(sk5[i][:, 0 : hi - lo], 5, lo, hi)

        def last2(i):
            lo, hi = parts[i]
            e2(5, lo, hi)
            store(5, lo, hi)

        last1(0)
        last1(1)
        last2(0)
        last1(2)
        last2(1)
        last2(2)
